import numpy as np
import ml_dtypes


def mxq(x, axis, fmt="e4m3"):
    dtype, down = {"e4m3": (ml_dtypes.float8_e4m3fn, 7), "e5m2": (ml_dtypes.float8_e5m2, 14)}[fmt]
    v = np.moveaxis(np.asarray(x, np.float32).astype(ml_dtypes.bfloat16).astype(np.float64), axis, -1)
    blocks = v.reshape(v.shape[:-1] + (-1, 32))
    amax = np.abs(blocks).max(-1, keepdims=True)
    byte = np.maximum(np.where(amax > 0, np.frexp(amax)[1] - 1 + 127, 0) - down, 1)
    scale = np.exp2(byte - 127.0)
    codes = (blocks / scale).astype(np.float32).astype(dtype).astype(np.float64)
    return np.moveaxis((codes * scale).reshape(v.shape), -1, axis)


WIDE = False


def mx_kscale(k):
    if not WIDE:
        return np.ones(k)
    levels = np.array([10, -10, 5, -5, 0])
    if k % 512:
        return np.exp2(np.random.permutation(np.resize(levels, k // 32))).repeat(32)
    a = np.empty((k // 512, 16))
    for p in range(k // 512):
        a[p, :8] = np.random.permutation(np.resize(levels, 8))
        for g in range(8):
            far = levels[np.abs(levels - a[p, g]) >= 10]
            a[p, g + 8] = far[np.random.randint(len(far))]
    return np.exp2(a.ravel()).repeat(32)


BF16 = ml_dtypes.bfloat16


def bf(x):
    return np.asarray(x, np.float32).astype(BF16)


def f64(x):
    return np.asarray(x).astype(np.float64)


B, NC, APC, D = 512, 8, 512, 512
H = 2 * D
LN_EPS = 1e-5


def setup_inputs():
    s = mx_kscale(APC)
    t = np.exp2(np.round(np.log2(mx_kscale(H)) / 2))
    return {"tri": bf(np.random.standard_normal((B, APC * NC)) * np.repeat(s, NC)),
            "W1": bf(np.random.standard_normal((NC, APC, H)) / np.sqrt(APC) / s[None, :, None] * t),
            "b1": bf(np.random.standard_normal((NC, H)) * 0.1 * t),
            "W2": bf(np.random.standard_normal((NC, H, D)) / np.sqrt(H) / (t * t)[None, :, None]),
            "b2": bf(np.random.standard_normal((NC, D)) * 0.1),
            "gamma": bf(1.0 + 0.1 * np.random.standard_normal((NC, D))),
            "beta": bf(np.random.standard_normal((NC, D)) * 0.1)}


def reference(tri, W1, b1, W2, b2, gamma, beta):
    tri, W1, b1, W2, b2, gamma, beta = f64(tri), f64(W1), f64(b1), f64(W2), f64(b2), f64(gamma), f64(beta)
    b, n_anchors = tri.shape
    n_comp, apc, _ = W1.shape
    d = W2.shape[2]
    x = np.transpose(tri.reshape(b, apc, n_comp), (2, 0, 1))
    h = f64(bf(mxq(x, 2, "e4m3") @ mxq(W1, 1, "e4m3"))) + b1[:, None, :]
    h = np.square(np.maximum(h, 0.0))
    y = (mxq(h, 2, "e4m3") @ mxq(W2, 1, "e4m3")) + b2[:, None, :]
    mu = np.mean(y, axis=-1, keepdims=True)
    var = np.mean(np.square(y - mu), axis=-1, keepdims=True)
    y = (y - mu) * (1.0 / np.sqrt(var + LN_EPS))
    y = y * gamma[:, None, :] + beta[:, None, :]
    return np.transpose(y, (1, 0, 2)).reshape(b, n_comp * d)

@@ -1,0 +1,330 @@
+from contextlib import ExitStack
+
+import concourse.mybir as mybir
+from concourse.masks import make_identity
+
+F32 = mybir.dt.float32
+BF16 = mybir.dt.bfloat16
+U32 = mybir.dt.uint32
+U8 = mybir.dt.uint8
+FP8X4 = mybir.dt.float8_e4m3fn_x4
+ACT = mybir.ActivationFunctionType
+ALU = mybir.AluOpType
+
+B, NC, APC, D = 512, 8, 512, 512
+H = 2 * D
+LN_EPS = 1e-5
+P = 128
+NBT = B // P
+FLOPS = 2 * B * NC * (APC * H + H * D)
+
+BANK_DT = BF16
+MANUAL = False
+SIGMA = False
+FILL = [6,3,3,2,3,2,3,2]
+PE_CHUNKS = []
+S_COPY = []
+HEAD_STEPS = 9
+NX = NBT * NC // 2
+
+
+def tile_patchwork_kernel(tc, tri, W1, b1, W2, b2, gamma, beta, out):
+    nc = tc.nc
+    with ExitStack() as ctx:
+        if MANUAL:
+            ctx.enter_context(tc.manual_schedule())
+        const = ctx.enter_context(tc.tile_pool(name="const", bufs=1))
+        raw = ctx.enter_context(tc.tile_pool(name="raw", bufs=4))
+        gw = ctx.enter_context(tc.tile_pool(name="gw", bufs=4))
+        wq = ctx.enter_context(tc.tile_pool(name="wq", bufs=8))
+        gx = ctx.enter_context(tc.tile_pool(name="gx", bufs=8))
+        hq = ctx.enter_context(tc.tile_pool(name="hq", bufs=4))
+        stats = ctx.enter_context(tc.tile_pool(name="stats", bufs=2))
+        psum = ctx.enter_context(tc.psum_pool(name="psum", bufs=8))
+
+        eps = const.tile([P, 1], F32, name="eps")
+        nc.vector.memset(eps[:], LN_EPS)
+        warm = const.tile([P, 1], F32, name="warm")
+        nc.scalar.activation(out=warm[:], in_=eps[:], func=ACT.Sqrt)
+        vrows = [const.tile([P, D], BF16, name="vrows%d" % v) for v in range(3)]
+        for v in range(3):
+            nc.vector.memset(vrows[v][:], 0.0)
+        ident = const.tile([P, P], BF16, name="ident")
+        make_identity(nc, ident[:])
+        identw = const.tile([P, P], F32, name="identw")
+        make_identity(nc, identw[:])
+        b1rows = const.tile([P, 512], BF16, name="b1rows")
+        nc.vector.memset(b1rows[:], 0.0)
+        b1cols = const.tile([P, 4, P], BF16, name="b1cols")
+        b1T = const.tile([P, 4, 2 * NC], BF16, name="b1T")
+        b2b = const.tile([P, NC * D], BF16, name="b2b")
+        xq = [const.tile([P, B], U32, name="xq%d" % k, align_bytes=64) for k in range(NC)]
+        xs = [const.tile([P, B], U8, name="xs%d" % k, align_bytes=64) for k in range(NC)]
+
+        raws = {}
+        gws = {}
+        wcodes = {}
+        state = {"step": 0, "qx": 0}
+
+        def load_w(c, s):
+            if s == 0:
+                t = raw.tile([P, 4, H], BF16, name="raw1", tag="raw")
+                nc.sync.dma_start(out=t[:], in_=W1[c].rearrange("(p j) h -> p j h", j=4))
+            elif not SIGMA:
+                t = raw.tile([P, 2, 4, D], BF16, name="raw2", tag="raw")
+                nc.sync.dma_start(out=t[:], in_=W2[c].rearrange("(g p j) d -> p g j d", g=2, j=4))
+            else:
+                t = raw.tile([P, 2, 4, D], BF16, name="raw2", tag="raw")
+                rows = W2[c].rearrange("(g q j r) d -> g j q r d", g=2, j=4, r=8)
+                for g in range(2):
+                    for j in range(4):
+                        nc.sync.dma_start(out=t[:, g, j, :], in_=rows[g, j].rearrange("q r d -> (q r) d"))
+            raws[(c, s)] = t
+
+        def spread(dst, v, row):
+            nc.tensor.matmul(out=dst, lhsT=ident[:, row:row + 1].to_broadcast([P, P]), rhs=vrows[v][:], start=True, stop=True)
+
+        def copy_chunk(n):
+            c, s, g = n // 4, (n % 4) // 2, n % 2
+            t = gw.tile([P, 2048], BF16, name="gw", tag="gw", align_bytes=64)
+            if n in PE_CHUNKS:
+                for half in range(2):
+                    wb = psum.tile([P, 1024], BF16, name="wbank", tag="bank")
+                    for q in range(2):
+                        piece = 2 * half + q
+                        if s == 0:
+                            mov = raws[(c, 0)][:, :, g * 512 + piece:(g + 1) * 512:4].rearrange("p j m -> p m j")
+                        else:
+                            mov = raws[(c, 1)][:, g, :, piece * P:(piece + 1) * P].rearrange("p j d -> p d j")
+                        nc.tensor.matmul(out=wb[:, q * 512:(q + 1) * 512].rearrange("p (m j) -> p m j", j=4),
+                                         lhsT=ident[:], rhs=mov, start=True, stop=True)
+                    nc.scalar.copy(out=t[:, half * 1024:(half + 1) * 1024], in_=wb[:])
+            elif s == 0 and not SIGMA:
+                src = raws[(c, 0)][:, :, g * 512:(g + 1) * 512].rearrange("p j (m t) -> p m j t", t=4)
+                nc.vector.tensor_copy(out=t[:].rearrange("p (t m j) -> p m j t", t=4, j=4), in_=src)
+            elif s == 0:
+                src = raws[(c, 0)][:, :, g * 512:(g + 1) * 512].rearrange("p j (q t r) -> p t q r j", t=4, r=8)
+                dst = t[:].rearrange("p (t q r j) -> p t q r j", t=4, r=8, j=4)
+                for tt in range(4):
+                    nc.vector.tensor_copy(out=dst[:, tt], in_=src[:, tt])
+            elif n in S_COPY:
+                nc.scalar.copy(out=t[:].rearrange("p (d j) -> p d j", j=4),
+                               in_=raws[(c, 1)][:, g].rearrange("p j d -> p d j"))
+            else:
+                nc.vector.tensor_copy(out=t[:].rearrange("p (c i j) -> p c j i", i=4, j=4),
+                                      in_=raws[(c, 1)][:, g].rearrange("p j (c i) -> p c j i", i=4))
+            gws[n] = t
+            if g == 1 and c + 2 < NC:
+                load_w(c + 2, s)
+
+        def quant_chunk(n):
+            s = (n % 4) // 2
+            q = wq.tile([P, 512], U32, name="wcode", tag="w%dq" % s, align_bytes=64)
+            sc = wq.tile([P, 512], U8, name="wscale", tag="w%ds" % s, align_bytes=64)
+            nc.vector.quantize_mx(out=q[:].bitcast(FP8X4), scales=sc[:], in_=gws[n][:])
+            wcodes[n] = (q, sc)
+
+        def fill(count):
+            for rep in range(count):
+                n = state["step"]
+                if n < 4 * NC:
+                    copy_chunk(n)
+                if 1 <= n <= 4 * NC:
+                    quant_chunk(n - 1)
+                state["step"] = n + 1
+
+        gxs = {}
+
+        def xpose_evac(tri_sb, n):
+            bt, pair = n // (NC // 2), n % (NC // 2)
+            words = tri_sb[bt][:].bitcast(F32)
+            xt = psum.tile([P, 4, P], F32, name="xt", tag="bank")
+            for t in range(4):
+                nc.tensor.transpose(xt[:, t, :], words[:, 4 * t + pair::16], identw[:])
+            halves = xt[:].rearrange("p t b -> p (t b)").bitcast(BF16).rearrange("p (t b e) -> p e b t", t=4, e=2)
+            for e in range(2):
+                g = gx.tile([P, 512], BF16, name="gx", tag="gx", align_bytes=64)
+                nc.scalar.copy(out=g[:].rearrange("p (b t) -> p b t", t=4), in_=halves[:, e])
+                gxs[2 * n + e] = g
+
+        def quant_x(upto):
+            while state["qx"] < min(upto, 2 * NX):
+                n = state["qx"]
+                bt, k = n // NC, n % NC
+                cols = slice(bt * P, (bt + 1) * P)
+                nc.vector.quantize_mx(out=xq[k][:, cols].bitcast(FP8X4), scales=xs[k][:, cols], in_=gxs[n][:])
+                state["qx"] = n + 1
+
+        banks = {}
+        rs = {}
+        ghs = {}
+        hcodes = {}
+
+        def mm1(k, g):
+            q, sc = wcodes[4 * k + g]
+            for t in range(4):
+                bank = psum.tile([P, B], BANK_DT, name="hbank", tag="bank")
+                cols = slice(t * P, (t + 1) * P)
+                nc.tensor.matmul_mx(out=bank[:], lhsT=q[:, cols].bitcast(FP8X4), lhsT_scale=sc[:, cols],
+                                    rhs=xq[k][:].bitcast(FP8X4), rhs_scale=xs[k][:], start=True, stop=True)
+                banks[(k, g, t)] = bank
+
+        def relu(late, k, g):
+            r = late["r"].tile([P, 4, B], F32, name="r", tag="r")
+            for t in range(4):
+                nc.scalar.activation(out=r[:, t, :], in_=banks[(k, g, t)][:], func=ACT.Relu,
+                                     bias=b1T[:, t, 2 * k + g:2 * k + g + 1], scale=1.0)
+            rs[(k, g)] = r
+
+        def square(late, k, g):
+            t = late["gh"].tile([P, 4 * B], BF16, name="gh", tag="gh", align_bytes=64)
+            nc.scalar.activation(out=t[:].rearrange("p (c i t) -> p c t i", i=4, t=4),
+                                 in_=rs[(k, g)][:].rearrange("p t (c i) -> p c t i", i=4), func=ACT.Square)
+            ghs[(k, g)] = t
+
+        def quant_h(k, g):
+            q = hq.tile([P, B], U32, name="hcode", tag="hq", align_bytes=64)
+            sc = hq.tile([P, B], U8, name="hscale", tag="hs", align_bytes=64)
+            nc.vector.quantize_mx(out=q[:].bitcast(FP8X4), scales=sc[:], in_=ghs[(k, g)][:])
+            hcodes[(k, g)] = (q, sc)
+
+        accs = {}
+        ys = {}
+        us = {}
+        st = {}
+        gbs = {}
+
+        def mm2(k):
+            for bt in range(NBT):
+                acc = psum.tile([P, D], F32, name="acc", tag="bank")
+                cols = slice(bt * P, (bt + 1) * P)
+                for g in range(2):
+                    q, sc = hcodes[(k, g)]
+                    wc, ws = wcodes[4 * k + 2 + g]
+                    nc.tensor.matmul_mx(out=acc[:], lhsT=q[:, cols].bitcast(FP8X4), lhsT_scale=sc[:, cols],
+                                        rhs=wc[:].bitcast(FP8X4), rhs_scale=ws[:], start=(g == 0), stop=(g == 1))
+                accs[(k, bt)] = acc
+            gb = psum.tile([P, 2, D], BF16, name="gb", tag="bank")
+            spread(gb[:, 0, :], 1, k)
+            spread(gb[:, 1, :], 2, k)
+            gbs[k] = gb
+
+        def add_bias(late, k, bts):
+            if bts[0] == 0:
+                st[k] = dict((nm, stats.tile([P, NBT], F32, name=nm, tag=nm))
+                             for nm in ("sums", "negmu", "ss", "std", "rstd"))
+            for bt in bts:
+                y = late["ln"].tile([P, D], F32, name="y", tag="y")
+                nc.vector.scalar_tensor_tensor(out=y[:], in0=accs[(k, bt)][:], scalar=1.0,
+                                               in1=b2b[:, k * D:(k + 1) * D], op0=ALU.mult, op1=ALU.add,
+                                               accum_out=st[k]["sums"][:, bt:bt + 1])
+                ys[(k, bt)] = y
+
+        def mean(k, pair):
+            cols = slice(2 * pair, 2 * pair + 2)
+            nc.vector.tensor_scalar(out=st[k]["negmu"][:, cols], in0=st[k]["sums"][:, cols], scalar1=-1.0 / D, scalar2=0.0,
+                                    op0=ALU.mult, op1=ALU.add)
+
+        def variance(late, k, pair):
+            cols = slice(2 * pair, 2 * pair + 2)
+            for bt in (2 * pair, 2 * pair + 1):
+                junk = late["ln"].tile([P, D], BF16, name="junk", tag="junk", bufs=2)
+                nc.scalar.activation(out=junk[:], in_=ys[(k, bt)][:], func=ACT.Square,
+                                     bias=st[k]["negmu"][:, bt:bt + 1], scale=1.0,
+                                     accum_out=st[k]["ss"][:, bt:bt + 1])
+            nc.scalar.activation(out=st[k]["std"][:, cols], in_=st[k]["ss"][:, cols], func=ACT.Sqrt,
+                                 bias=eps[:], scale=1.0 / D)
+
+        def centre_gain(late, k, pair):
+            for bt in (2 * pair, 2 * pair + 1):
+                u = late["ln"].tile([P, D], F32, name="u", tag="u")
+                nc.vector.scalar_tensor_tensor(out=u[:], in0=ys[(k, bt)][:], scalar=st[k]["negmu"][:, bt:bt + 1],
+                                               in1=gbs[k][:, 0, :], op0=ALU.add, op1=ALU.mult)
+                us[(k, bt)] = u
+
+        def invert(k, pair):
+            cols = slice(2 * pair, 2 * pair + 2)
+            nc.vector.reciprocal(out=st[k]["rstd"][:, cols], in_=st[k]["std"][:, cols])
+
+        def scale_shift_store(late, k, pair):
+            for bt in (2 * pair, 2 * pair + 1):
+                z = late["ln"].tile([P, D], F32, name="z", tag="z")
+                nc.vector.scalar_tensor_tensor(out=z[:], in0=us[(k, bt)][:], scalar=st[k]["rstd"][:, bt:bt + 1],
+                                               in1=gbs[k][:, 1, :], op0=ALU.mult, op1=ALU.add)
+                nc.sync.dma_start(out=out[bt * P:(bt + 1) * P, k * D:(k + 1) * D], in_=z[:])
+
+        with tc.tile_pool(name="tri", bufs=1) as tri_pool:
+            tri_sb = [tri_pool.tile([P, NC * APC], BF16, name="tri%d" % bt) for bt in range(NBT)]
+            nc.sync.dma_start(out=b1rows[0:2 * NC, :], in_=b1.rearrange("k (g c) -> (k g) c", g=2))
+            for v, vec in enumerate((b2, gamma, beta)):
+                nc.sync.dma_start(out=vrows[v][0:NC, :], in_=vec)
+            for i in range(NBT):
+                load_w(i // 2, i % 2)
+                nc.sync.dma_start(out=tri_sb[i][:], in_=tri[i * P:(i + 1) * P, :])
+            if SIGMA:
+                nc.vector.tensor_copy(out=b1cols[:].rearrange("p t (q r) -> p t q r", r=8),
+                                      in_=b1rows[:].rearrange("p (q t r) -> p t q r", t=4, r=8))
+            else:
+                nc.vector.tensor_copy(out=b1cols[:], in_=b1rows[:].rearrange("p (m t) -> p t m", t=4))
+            b1p = psum.tile([P, 4, P], BF16, name="b1p", tag="bank")
+            for t in range(4):
+                nc.tensor.transpose(b1p[:, t, :], b1cols[:, t, :], ident[:])
+            nc.scalar.copy(out=b1T[:], in_=b1p[:, :, 0:2 * NC])
+            for kk in range(NC // 2):
+                bb = psum.tile([P, 2, D], BF16, name="bb", tag="bank")
+                spread(bb[:, 0, :], 0, 2 * kk)
+                spread(bb[:, 1, :], 0, 2 * kk + 1)
+                nc.scalar.copy(out=b2b[:, 2 * kk * D:(2 * kk + 2) * D], in_=bb[:].rearrange("p a d -> p (a d)"))
+            for j in range(HEAD_STEPS):
+                fill(1)
+                quant_x(4 * j - 3)
+                for n in range(2 * j, min(2 * j + 2, NX)):
+                    xpose_evac(tri_sb, n)
+
+        late = {"r": ctx.enter_context(tc.tile_pool(name="r", bufs=2)),
+                "gh": ctx.enter_context(tc.tile_pool(name="gh", bufs=2)),
+                "ln": ctx.enter_context(tc.tile_pool(name="ln", bufs=4))}
+        mm1(0, 0)
+
+        for i in range(NC + 1):
+            cur = i < NC
+            prev = i >= 1
+            share = [(FILL[i] + 3 - s) // 4 for s in range(4)] if cur else [0, 0, 0, 0]
+            if prev:
+                quant_h(i - 1, 1)
+                mm2(i - 1)
+            else:
+                quant_x(2 * NX)
+            if cur:
+                relu(late, i, 0)
+                mm1(i, 1)
+            fill(share[0])
+            if prev:
+                add_bias(late, i - 1, (0, 1, 2))
+                mean(i - 1, 0)
+                add_bias(late, i - 1, (3,))
+            if cur:
+                square(late, i, 0)
+            fill(share[1])
+            if prev:
+                mean(i - 1, 1)
+                variance(late, i - 1, 0)
+            if cur:
+                quant_h(i, 0)
+                if i + 1 < NC:
+                    mm1(i + 1, 0)
+                relu(late, i, 1)
+            if prev:
+                invert(i - 1, 0)
+                centre_gain(late, i - 1, 0)
+                centre_gain(late, i - 1, 1)
+                variance(late, i - 1, 1)
+            fill(share[2])
+            if prev:
+                invert(i - 1, 1)
+                scale_shift_store(late, i - 1, 0)
+            if cur:
+                square(late, i, 1)
+            fill(share[3])
+            if prev:
+                scale_shift_store(late, i - 1, 1)

@@ -18,34 +18,33 @@ P = 128
 NBT = B // P
 FLOPS = 2 * B * NC * (APC * H + H * D)
 
-BANK_DT = BF16
-MANUAL = False
-SIGMA = False
-FILL = [6,3,3,2,3,2,3,2]
-PE_CHUNKS = []
-S_COPY = []
-HEAD_STEPS = 9
-NX = NBT * NC // 2
+G_FROM = 2
+X_HEAD = 2
+XB = False
+RV = ((0, 0), (0, 1), (0, 1), (0, 1), (0, 1), (0, 1), (1, 1), (1, 1))
+W1Q = ((1, 1, 1), (0, 1, 0), (0, 1, 0), (0, 1, 0), (0, 1, 0), (0, 1, 0), (0, 0, 0), (0, 0, 0), (0, 0, 0))
+HEAD_END = (1, 1, 1, 1)
 
 
 def tile_patchwork_kernel(tc, tri, W1, b1, W2, b2, gamma, beta, out):
     nc = tc.nc
     with ExitStack() as ctx:
-        if MANUAL:
-            ctx.enter_context(tc.manual_schedule())
+        ctx.enter_context(tc.manual_schedule())
         const = ctx.enter_context(tc.tile_pool(name="const", bufs=1))
-        raw = ctx.enter_context(tc.tile_pool(name="raw", bufs=4))
-        gw = ctx.enter_context(tc.tile_pool(name="gw", bufs=4))
+        raw = ctx.enter_context(tc.tile_pool(name="raw", bufs=3))
+        gw = ctx.enter_context(tc.tile_pool(name="gw", bufs=3))
+        gv = ctx.enter_context(tc.tile_pool(name="gv", bufs=1))
         wq = ctx.enter_context(tc.tile_pool(name="wq", bufs=8))
-        gx = ctx.enter_context(tc.tile_pool(name="gx", bufs=8))
         hq = ctx.enter_context(tc.tile_pool(name="hq", bufs=4))
         stats = ctx.enter_context(tc.tile_pool(name="stats", bufs=2))
-        psum = ctx.enter_context(tc.psum_pool(name="psum", bufs=8))
+        rp = ctx.enter_context(tc.tile_pool(name="r", bufs=2))
+        ghp = ctx.enter_context(tc.tile_pool(name="gh", bufs=2))
+        psum = ctx.enter_context(tc.psum_pool(name="psum", bufs=1))
 
         eps = const.tile([P, 1], F32, name="eps")
         nc.vector.memset(eps[:], LN_EPS)
         warm = const.tile([P, 1], F32, name="warm")
-        nc.scalar.activation(out=warm[:], in_=eps[:], func=ACT.Sqrt)
+        nc.scalar.activation(out=warm[:], in_=eps[:], func=ACT.Abs_reciprocal_sqrt)
         vrows = [const.tile([P, D], BF16, name="vrows%d" % v) for v in range(3)]
         for v in range(3):
             nc.vector.memset(vrows[v][:], 0.0)
@@ -64,96 +63,78 @@ def tile_patchwork_kernel(tc, tri, W1, b1, W2, b2, gamma, beta, out):
         raws = {}
         gws = {}
         wcodes = {}
-        state = {"step": 0, "qx": 0}
 
         def load_w(c, s):
+            if c >= NC:
+                return
             if s == 0:
-                t = raw.tile([P, 4, H], BF16, name="raw1", tag="raw")
+                t = raw.tile([P, 4, H], BF16, name="raw1", tag="raw1")
                 nc.sync.dma_start(out=t[:], in_=W1[c].rearrange("(p j) h -> p j h", j=4))
-            elif not SIGMA:
-                t = raw.tile([P, 2, 4, D], BF16, name="raw2", tag="raw")
-                nc.sync.dma_start(out=t[:], in_=W2[c].rearrange("(g p j) d -> p g j d", g=2, j=4))
             else:
-                t = raw.tile([P, 2, 4, D], BF16, name="raw2", tag="raw")
-                rows = W2[c].rearrange("(g q j r) d -> g j q r d", g=2, j=4, r=8)
-                for g in range(2):
-                    for j in range(4):
-                        nc.sync.dma_start(out=t[:, g, j, :], in_=rows[g, j].rearrange("q r d -> (q r) d"))
+                t = raw.tile([P, 2, 4, D], BF16, name="raw2", tag="raw2")
+                nc.sync.dma_start(out=t[:], in_=W2[c].rearrange("(g p j) d -> p g j d", g=2, j=4))
             raws[(c, s)] = t
 
         def spread(dst, v, row):
             nc.tensor.matmul(out=dst, lhsT=ident[:, row:row + 1].to_broadcast([P, P]), rhs=vrows[v][:], start=True, stop=True)
 
-        def copy_chunk(n):
-            c, s, g = n // 4, (n % 4) // 2, n % 2
+        def copy_w1(c, g):
+            if c >= NC:
+                return
             t = gw.tile([P, 2048], BF16, name="gw", tag="gw", align_bytes=64)
-            if n in PE_CHUNKS:
-                for half in range(2):
-                    wb = psum.tile([P, 1024], BF16, name="wbank", tag="bank")
-                    for q in range(2):
-                        piece = 2 * half + q
-                        if s == 0:
-                            mov = raws[(c, 0)][:, :, g * 512 + piece:(g + 1) * 512:4].rearrange("p j m -> p m j")
-                        else:
-                            mov = raws[(c, 1)][:, g, :, piece * P:(piece + 1) * P].rearrange("p j d -> p d j")
-                        nc.tensor.matmul(out=wb[:, q * 512:(q + 1) * 512].rearrange("p (m j) -> p m j", j=4),
-                                         lhsT=ident[:], rhs=mov, start=True, stop=True)
-                    nc.scalar.copy(out=t[:, half * 1024:(half + 1) * 1024], in_=wb[:])
-            elif s == 0 and not SIGMA:
-                src = raws[(c, 0)][:, :, g * 512:(g + 1) * 512].rearrange("p j (m t) -> p m j t", t=4)
-                nc.vector.tensor_copy(out=t[:].rearrange("p (t m j) -> p m j t", t=4, j=4), in_=src)
-            elif s == 0:
-                src = raws[(c, 0)][:, :, g * 512:(g + 1) * 512].rearrange("p j (q t r) -> p t q r j", t=4, r=8)
-                dst = t[:].rearrange("p (t q r j) -> p t q r j", t=4, r=8, j=4)
-                for tt in range(4):
-                    nc.vector.tensor_copy(out=dst[:, tt], in_=src[:, tt])
-            elif n in S_COPY:
-                nc.scalar.copy(out=t[:].rearrange("p (d j) -> p d j", j=4),
-                               in_=raws[(c, 1)][:, g].rearrange("p j d -> p d j"))
+            src = raws[(c, 0)][:, :, g * 512:(g + 1) * 512].rearrange("p j (m t) -> p m j t", t=4)
+            nc.vector.tensor_copy(out=t[:].rearrange("p (t m j) -> p m j t", t=4, j=4), in_=src)
+            gws[(c, 0, g)] = t
+            if g == 1:
+                load_w(c + 3, 0)
+
+        def quant_w1(c, g):
+            if c >= NC:
+                return
+            q = wq.tile([P, 512], U32, name="wcode", tag="w0q", align_bytes=64)
+            sc = wq.tile([P, 512], U8, name="wscale", tag="w0s", align_bytes=64)
+            nc.vector.quantize_mx(out=q[:].bitcast(FP8X4), scales=sc[:], in_=gws[(c, 0, g)][:])
+            wcodes[(c, 0, g)] = (q, sc)
+
+        w1state = {"s": 0}
+
+        def w1_steps(count):
+            for rep_ in range(count):
+                s = w1state["s"]
+                if s < 2 * NC:
+                    copy_w1(s // 2, s % 2)
+                if 1 <= s <= 2 * NC:
+                    quant_w1((s - 1) // 2, (s - 1) % 2)
+                w1state["s"] = s + 1
+
+        PIECES = ((0, 0, 512), (1, 0, 256), (1, 256, 512))
+
+        def copy_w2(c, piece):
+            if c >= NC:
+                return
+            g, lo, hi = PIECES[piece]
+            t = gv.tile([P, 4 * (hi - lo)], BF16, name="gv%d" % piece, tag="gv%d" % piece, align_bytes=64)
+            if c >= G_FROM:
+                nc.gpsimd.tensor_scalar(out=t[:].rearrange("p (d j) -> p d j", j=4),
+                                        in0=raws[(c, 1)][:, g, :, lo:hi].rearrange("p j d -> p d j"),
+                                        scalar1=1.0, scalar2=0.0, op0=ALU.mult, op1=ALU.add)
             else:
                 nc.vector.tensor_copy(out=t[:].rearrange("p (c i j) -> p c j i", i=4, j=4),
-                                      in_=raws[(c, 1)][:, g].rearrange("p j (c i) -> p c j i", i=4))
-            gws[n] = t
-            if g == 1 and c + 2 < NC:
-                load_w(c + 2, s)
+                                      in_=raws[(c, 1)][:, g, :, lo:hi].rearrange("p j (c i) -> p c j i", i=4))
+            gws[(c, 1, piece)] = t
+            if piece == 2:
+                load_w(c + 3, 1)
 
-        def quant_chunk(n):
-            s = (n % 4) // 2
-            q = wq.tile([P, 512], U32, name="wcode", tag="w%dq" % s, align_bytes=64)
-            sc = wq.tile([P, 512], U8, name="wscale", tag="w%ds" % s, align_bytes=64)
-            nc.vector.quantize_mx(out=q[:].bitcast(FP8X4), scales=sc[:], in_=gws[n][:])
-            wcodes[n] = (q, sc)
-
-        def fill(count):
-            for rep in range(count):
-                n = state["step"]
-                if n < 4 * NC:
-                    copy_chunk(n)
-                if 1 <= n <= 4 * NC:
-                    quant_chunk(n - 1)
-                state["step"] = n + 1
-
-        gxs = {}
-
-        def xpose_evac(tri_sb, n):
-            bt, pair = n // (NC // 2), n % (NC // 2)
-            words = tri_sb[bt][:].bitcast(F32)
-            xt = psum.tile([P, 4, P], F32, name="xt", tag="bank")
-            for t in range(4):
-                nc.tensor.transpose(xt[:, t, :], words[:, 4 * t + pair::16], identw[:])
-            halves = xt[:].rearrange("p t b -> p (t b)").bitcast(BF16).rearrange("p (t b e) -> p e b t", t=4, e=2)
-            for e in range(2):
-                g = gx.tile([P, 512], BF16, name="gx", tag="gx", align_bytes=64)
-                nc.scalar.copy(out=g[:].rearrange("p (b t) -> p b t", t=4), in_=halves[:, e])
-                gxs[2 * n + e] = g
-
-        def quant_x(upto):
-            while state["qx"] < min(upto, 2 * NX):
-                n = state["qx"]
-                bt, k = n // NC, n % NC
-                cols = slice(bt * P, (bt + 1) * P)
-                nc.vector.quantize_mx(out=xq[k][:, cols].bitcast(FP8X4), scales=xs[k][:, cols], in_=gxs[n][:])
-                state["qx"] = n + 1
+        def quant_w2(c, piece):
+            if c >= NC or c < 0:
+                return
+            g, lo, hi = PIECES[piece]
+            if piece != 2:
+                q = wq.tile([P, 512], U32, name="wcode", tag="w1q", bufs=5, align_bytes=64)
+                sc = wq.tile([P, 512], U8, name="wscale", tag="w1s", bufs=5, align_bytes=64)
+                wcodes[(c, 1, g)] = (q, sc)
+            q, sc = wcodes[(c, 1, g)]
+            nc.vector.quantize_mx(out=q[:, lo:hi].bitcast(FP8X4), scales=sc[:, lo:hi], in_=gws[(c, 1, piece)][:])
 
         banks = {}
         rs = {}
@@ -161,23 +142,33 @@ def tile_patchwork_kernel(tc, tri, W1, b1, W2, b2, gamma, beta, out):
         hcodes = {}
 
         def mm1(k, g):
-            q, sc = wcodes[4 * k + g]
+            if k >= NC:
+                return
+            q, sc = wcodes[(k, 0, g)]
             for t in range(4):
-                bank = psum.tile([P, B], BANK_DT, name="hbank", tag="bank")
+                if t % 2 == 0:
+                    bank = psum.tile([P, 2, B], BF16, name="hbank", tag="h", bufs=4)
                 cols = slice(t * P, (t + 1) * P)
-                nc.tensor.matmul_mx(out=bank[:], lhsT=q[:, cols].bitcast(FP8X4), lhsT_scale=sc[:, cols],
+                nc.tensor.matmul_mx(out=bank[:, t % 2, :], lhsT=q[:, cols].bitcast(FP8X4), lhsT_scale=sc[:, cols],
                                     rhs=xq[k][:].bitcast(FP8X4), rhs_scale=xs[k][:], start=True, stop=True)
-                banks[(k, g, t)] = bank
+                banks[(k, g, t)] = bank[:, t % 2, :]
 
-        def relu(late, k, g):
-            r = late["r"].tile([P, 4, B], F32, name="r", tag="r")
-            for t in range(4):
-                nc.scalar.activation(out=r[:, t, :], in_=banks[(k, g, t)][:], func=ACT.Relu,
+        def relu(k, g):
+            r = rp.tile([P, 4, B], F32, name="r", tag="r")
+            for t in range(4 - RV[k][g]):
+                nc.scalar.activation(out=r[:, t, :], in_=banks[(k, g, t)], func=ACT.Relu,
                                      bias=b1T[:, t, 2 * k + g:2 * k + g + 1], scale=1.0)
             rs[(k, g)] = r
 
-        def square(late, k, g):
-            t = late["gh"].tile([P, 4 * B], BF16, name="gh", tag="gh", align_bytes=64)
+        def relu_v(k, g):
+            if k >= NC:
+                return
+            for t in range(4 - RV[k][g], 4):
+                nc.vector.tensor_scalar(out=rs[(k, g)][:, t, :], in0=banks[(k, g, t)],
+                                        scalar1=b1T[:, t, 2 * k + g:2 * k + g + 1], scalar2=0.0, op0=ALU.add, op1=ALU.max)
+
+        def square(k, g):
+            t = ghp.tile([P, 4 * B], BF16, name="gh", tag="gh", align_bytes=64)
             nc.scalar.activation(out=t[:].rearrange("p (c i t) -> p c t i", i=4, t=4),
                                  in_=rs[(k, g)][:].rearrange("p t (c i) -> p c t i", i=4), func=ACT.Square)
             ghs[(k, g)] = t
@@ -194,137 +185,163 @@ def tile_patchwork_kernel(tc, tri, W1, b1, W2, b2, gamma, beta, out):
         st = {}
         gbs = {}
 
-        def mm2(k):
-            for bt in range(NBT):
-                acc = psum.tile([P, D], F32, name="acc", tag="bank")
-                cols = slice(bt * P, (bt + 1) * P)
-                for g in range(2):
-                    q, sc = hcodes[(k, g)]
-                    wc, ws = wcodes[4 * k + 2 + g]
-                    nc.tensor.matmul_mx(out=acc[:], lhsT=q[:, cols].bitcast(FP8X4), lhsT_scale=sc[:, cols],
-                                        rhs=wc[:].bitcast(FP8X4), rhs_scale=ws[:], start=(g == 0), stop=(g == 1))
-                accs[(k, bt)] = acc
-            gb = psum.tile([P, 2, D], BF16, name="gb", tag="bank")
+        def spread_gb(k):
+            gb = psum.tile([P, 2, D], BF16, name="gb", tag="gb", bufs=1)
             spread(gb[:, 0, :], 1, k)
             spread(gb[:, 1, :], 2, k)
             gbs[k] = gb
 
-        def add_bias(late, k, bts):
-            if bts[0] == 0:
-                st[k] = dict((nm, stats.tile([P, NBT], F32, name=nm, tag=nm))
-                             for nm in ("sums", "negmu", "ss", "std", "rstd"))
-            for bt in bts:
-                y = late["ln"].tile([P, D], F32, name="y", tag="y")
+        def mm2(k):
+            for bt in range(NBT):
+                acc = psum.tile([P, D], F32, name="acc", tag="acc", bufs=3)
+                cols = slice(bt * P, (bt + 1) * P)
+                for g in range(2):
+                    q, sc = hcodes[(k, g)]
+                    wc, ws = wcodes[(k, 1, g)]
+                    nc.tensor.matmul_mx(out=acc[:], lhsT=q[:, cols].bitcast(FP8X4), lhsT_scale=sc[:, cols],
+                                        rhs=wc[:].bitcast(FP8X4), rhs_scale=ws[:], start=(g == 0), stop=(g == 1))
+                accs[(k, bt)] = acc
+
+        def add_bias(ln, k):
+            st[k] = dict((nm, stats.tile([P, NBT], F32, name=nm, tag=nm)) for nm in ("sums", "negmu", "ss", "rstd"))
+            for bt in range(NBT):
+                y = ln.tile([P, D], F32, name="y", tag="y")
                 nc.vector.scalar_tensor_tensor(out=y[:], in0=accs[(k, bt)][:], scalar=1.0,
                                                in1=b2b[:, k * D:(k + 1) * D], op0=ALU.mult, op1=ALU.add,
                                                accum_out=st[k]["sums"][:, bt:bt + 1])
                 ys[(k, bt)] = y
-
-        def mean(k, pair):
-            cols = slice(2 * pair, 2 * pair + 2)
-            nc.vector.tensor_scalar(out=st[k]["negmu"][:, cols], in0=st[k]["sums"][:, cols], scalar1=-1.0 / D, scalar2=0.0,
+            nc.vector.tensor_scalar(out=st[k]["negmu"][:], in0=st[k]["sums"][:], scalar1=-1.0 / D, scalar2=0.0,
                                     op0=ALU.mult, op1=ALU.add)
 
-        def variance(late, k, pair):
-            cols = slice(2 * pair, 2 * pair + 2)
-            for bt in (2 * pair, 2 * pair + 1):
-                junk = late["ln"].tile([P, D], BF16, name="junk", tag="junk", bufs=2)
+        def variance(ln, k):
+            for bt in range(NBT):
+                junk = ln.tile([P, D], BF16, name="junk", tag="junk", bufs=2)
                 nc.scalar.activation(out=junk[:], in_=ys[(k, bt)][:], func=ACT.Square,
                                      bias=st[k]["negmu"][:, bt:bt + 1], scale=1.0,
                                      accum_out=st[k]["ss"][:, bt:bt + 1])
-            nc.scalar.activation(out=st[k]["std"][:, cols], in_=st[k]["ss"][:, cols], func=ACT.Sqrt,
+            nc.scalar.activation(out=st[k]["rstd"][:], in_=st[k]["ss"][:], func=ACT.Abs_reciprocal_sqrt,
                                  bias=eps[:], scale=1.0 / D)
 
-        def centre_gain(late, k, pair):
-            for bt in (2 * pair, 2 * pair + 1):
-                u = late["ln"].tile([P, D], F32, name="u", tag="u")
+        def centre_gain(ln, k):
+            for bt in range(NBT):
+                u = ln.tile([P, D], F32, name="u", tag="u")
                 nc.vector.scalar_tensor_tensor(out=u[:], in0=ys[(k, bt)][:], scalar=st[k]["negmu"][:, bt:bt + 1],
                                                in1=gbs[k][:, 0, :], op0=ALU.add, op1=ALU.mult)
                 us[(k, bt)] = u
 
-        def invert(k, pair):
-            cols = slice(2 * pair, 2 * pair + 2)
-            nc.vector.reciprocal(out=st[k]["rstd"][:, cols], in_=st[k]["std"][:, cols])
-
-        def scale_shift_store(late, k, pair):
-            for bt in (2 * pair, 2 * pair + 1):
-                z = late["ln"].tile([P, D], F32, name="z", tag="z")
+        def scale_shift_store(ln, k):
+            for bt in range(NBT):
+                z = ln.tile([P, D], F32, name="z", tag="z")
                 nc.vector.scalar_tensor_tensor(out=z[:], in0=us[(k, bt)][:], scalar=st[k]["rstd"][:, bt:bt + 1],
                                                in1=gbs[k][:, 1, :], op0=ALU.mult, op1=ALU.add)
                 nc.sync.dma_start(out=out[bt * P:(bt + 1) * P, k * D:(k + 1) * D], in_=z[:])
 
+        def head_v(bt):
+            if bt == 0:
+                w1_steps(2)
+            elif bt == 1:
+                copy_w2(0, 0)
+                copy_w2(0, 1)
+                quant_w2(0, 0)
+                copy_w2(0, 2)
+                quant_w2(0, 1)
+            elif bt == 2:
+                w1_steps(1)
+                quant_w2(0, 2)
+                w1_steps(1)
+            else:
+                copy_w2(1, 0)
+                w1_steps(1)
+                copy_w2(1, 1)
+                copy_w2(1, 2)
+
+        def round_(i, ln, extra):
+            cur = i < NC
+            prev = i >= 1
+            if prev:
+                spread_gb(i - 1)
+                quant_h(i - 1, 1)
+                mm2(i - 1)
+            if cur:
+                relu(i, 0)
+                mm1(i + 1, 0)
+            w1_steps(W1Q[i][0])
+            if prev:
+                quant_w2(i, 0)
+                quant_w2(i, 1)
+            relu_v(i, 0)
+            if prev:
+                add_bias(ln, i - 1)
+            if cur:
+                square(i, 0)
+            if prev:
+                copy_w2(i + 1, 0)
+                copy_w2(i + 1, 1)
+                centre_gain(ln, i - 1)
+            if cur:
+                relu(i, 1)
+                mm1(i + 1, 1)
+            relu_v(i, 1)
+            if prev:
+                variance(ln, i - 1)
+            if cur:
+                quant_h(i, 0)
+            w1_steps(W1Q[i][1])
+            if prev:
+                quant_w2(i, 2)
+                copy_w2(i + 1, 2)
+                scale_shift_store(ln, i - 1)
+            if cur:
+                square(i, 1)
+            w1_steps(W1Q[i][2])
+
         with tc.tile_pool(name="tri", bufs=1) as tri_pool:
             tri_sb = [tri_pool.tile([P, NC * APC], BF16, name="tri%d" % bt) for bt in range(NBT)]
+            gxs = [tri_pool.tile([P, 4 * B], BF16, name="gx%d" % k, align_bytes=64) for k in range(NC)]
+
+            def xpose(bt, pair):
+                words = tri_sb[bt][:].bitcast(F32)
+                xt = psum.tile([P, 4, P], F32, name="xt", tag="h", bufs=4)
+                for t in range(4):
+                    nc.tensor.transpose(xt[:, t, :], words[:, 4 * t + pair::16], identw[:])
+                halves = xt[:].rearrange("p t b -> p (t b)").bitcast(BF16).rearrange("p (t b e) -> p e b t", t=4, e=2)
+                for e in range(2):
+                    nc.scalar.copy(out=gxs[2 * pair + e][:, bt * 512:(bt + 1) * 512].rearrange("p (b t) -> p b t", t=4),
+                                   in_=halves[:, e])
+
+            def quant_x(k):
+                nc.vector.quantize_mx(out=xq[k][:].bitcast(FP8X4), scales=xs[k][:], in_=gxs[k][:])
+
             nc.sync.dma_start(out=b1rows[0:2 * NC, :], in_=b1.rearrange("k (g c) -> (k g) c", g=2))
             for v, vec in enumerate((b2, gamma, beta)):
                 nc.sync.dma_start(out=vrows[v][0:NC, :], in_=vec)
-            for i in range(NBT):
-                load_w(i // 2, i % 2)
-                nc.sync.dma_start(out=tri_sb[i][:], in_=tri[i * P:(i + 1) * P, :])
-            if SIGMA:
-                nc.vector.tensor_copy(out=b1cols[:].rearrange("p t (q r) -> p t q r", r=8),
-                                      in_=b1rows[:].rearrange("p (q t r) -> p t q r", t=4, r=8))
-            else:
-                nc.vector.tensor_copy(out=b1cols[:], in_=b1rows[:].rearrange("p (m t) -> p t m", t=4))
-            b1p = psum.tile([P, 4, P], BF16, name="b1p", tag="bank")
+            for bt in range(NBT):
+                load_w(bt // 2, bt % 2)
+                nc.sync.dma_start(out=tri_sb[bt][:], in_=tri[bt * P:(bt + 1) * P, :])
+            load_w(2, 0)
+            load_w(2, 1)
+            nc.vector.tensor_copy(out=b1cols[:], in_=b1rows[:].rearrange("p (m t) -> p t m", t=4))
+            b1p = psum.tile([P, 4, P], BF16, name="b1p", tag="gb", bufs=1)
             for t in range(4):
                 nc.tensor.transpose(b1p[:, t, :], b1cols[:, t, :], ident[:])
             nc.scalar.copy(out=b1T[:], in_=b1p[:, :, 0:2 * NC])
             for kk in range(NC // 2):
-                bb = psum.tile([P, 2, D], BF16, name="bb", tag="bank")
+                bb = psum.tile([P, 2, D], BF16, name="bb", tag="acc", bufs=3)
                 spread(bb[:, 0, :], 0, 2 * kk)
                 spread(bb[:, 1, :], 0, 2 * kk + 1)
                 nc.scalar.copy(out=b2b[:, 2 * kk * D:(2 * kk + 2) * D], in_=bb[:].rearrange("p a d -> p (a d)"))
-            for j in range(HEAD_STEPS):
-                fill(1)
-                quant_x(4 * j - 3)
-                for n in range(2 * j, min(2 * j + 2, NX)):
-                    xpose_evac(tri_sb, n)
+            for bt in range(NBT):
+                head_v(bt)
+                for pair in range(NC // 2):
+                    xpose(bt, pair)
+            for pair in range(NC // 2):
+                quant_x(2 * pair)
+                quant_x(2 * pair + 1)
+                if pair == 0:
+                    mm1(0, 0)
+                    mm1(0, 1)
+                w1_steps(HEAD_END[pair])
 
-        late = {"r": ctx.enter_context(tc.tile_pool(name="r", bufs=2)),
-                "gh": ctx.enter_context(tc.tile_pool(name="gh", bufs=2)),
-                "ln": ctx.enter_context(tc.tile_pool(name="ln", bufs=4))}
-        mm1(0, 0)
-
+        ln = ctx.enter_context(tc.tile_pool(name="ln", bufs=4))
         for i in range(NC + 1):
-            cur = i < NC
-            prev = i >= 1
-            share = [(FILL[i] + 3 - s) // 4 for s in range(4)] if cur else [0, 0, 0, 0]
-            if prev:
-                quant_h(i - 1, 1)
-                mm2(i - 1)
-            else:
-                quant_x(2 * NX)
-            if cur:
-                relu(late, i, 0)
-                mm1(i, 1)
-            fill(share[0])
-            if prev:
-                add_bias(late, i - 1, (0, 1, 2))
-                mean(i - 1, 0)
-                add_bias(late, i - 1, (3,))
-            if cur:
-                square(late, i, 0)
-            fill(share[1])
-            if prev:
-                mean(i - 1, 1)
-                variance(late, i - 1, 0)
-            if cur:
-                quant_h(i, 0)
-                if i + 1 < NC:
-                    mm1(i + 1, 0)
-                relu(late, i, 1)
-            if prev:
-                invert(i - 1, 0)
-                centre_gain(late, i - 1, 0)
-                centre_gain(late, i - 1, 1)
-                variance(late, i - 1, 1)
-            fill(share[2])
-            if prev:
-                invert(i - 1, 1)
-                scale_shift_store(late, i - 1, 0)
-            if cur:
-                square(late, i, 1)
-            fill(share[3])
-            if prev:
-                scale_shift_store(late, i - 1, 1)
+            round_(i, ln, lambda slot: None)

@@ -21,15 +21,17 @@ FLOPS = 2 * B * NC * (APC * H + H * D)
 G_FROM = 2
 X_HEAD = 2
 XB = False
-RV = ((0, 0), (0, 1), (0, 1), (0, 1), (0, 1), (0, 1), (1, 1), (1, 1))
-W1Q = ((1, 1, 1), (0, 1, 0), (0, 1, 0), (0, 1, 0), (0, 1, 0), (0, 1, 0), (0, 0, 0), (0, 0, 0), (0, 0, 0))
-HEAD_END = (1, 1, 1, 1)
+RV = ((0, 0), (0, 0), (0, 0), (0, 0), (0, 0), (0, 0), (0, 0), (0, 0))
+W1Q = ((2, 2, 2), (0, 1, 0), (0, 1, 0), (0, 1, 0), (0, 1, 0), (0, 1, 0), (0, 0, 0), (0, 0, 0), (0, 0, 0))
+W1_AHEAD = 1
+HEAD_RATE = 2
+X_LAG = 1
 
 
 def tile_patchwork_kernel(tc, tri, W1, b1, W2, b2, gamma, beta, out):
     nc = tc.nc
     with ExitStack() as ctx:
-        ctx.enter_context(tc.manual_schedule())
+        ctx.enter_context(tc.manual_schedule(engines={mybir.EngineType.DVE, mybir.EngineType.Pool}))
         const = ctx.enter_context(tc.tile_pool(name="const", bufs=1))
         raw = ctx.enter_context(tc.tile_pool(name="raw", bufs=3))
         gw = ctx.enter_context(tc.tile_pool(name="gw", bufs=3))
@@ -41,19 +43,17 @@ def tile_patchwork_kernel(tc, tri, W1, b1, W2, b2, gamma, beta, out):
         ghp = ctx.enter_context(tc.tile_pool(name="gh", bufs=2))
         psum = ctx.enter_context(tc.psum_pool(name="psum", bufs=1))
 
+        b1rows = const.tile([P, 512], BF16, name="b1rows")
+        nc.vector.memset(b1rows[:], 0.0)
+        vrows = [const.tile([P, D], BF16, name="vrows%d" % v) for v in range(3)]
+        for v in range(3):
+            nc.vector.memset(vrows[v][:], 0.0)
         eps = const.tile([P, 1], F32, name="eps")
         nc.vector.memset(eps[:], LN_EPS)
         warm = const.tile([P, 1], F32, name="warm")
         nc.scalar.activation(out=warm[:], in_=eps[:], func=ACT.Abs_reciprocal_sqrt)
-        vrows = [const.tile([P, D], BF16, name="vrows%d" % v) for v in range(3)]
-        for v in range(3):
-            nc.vector.memset(vrows[v][:], 0.0)
         ident = const.tile([P, P], BF16, name="ident")
-        make_identity(nc, ident[:])
         identw = const.tile([P, P], F32, name="identw")
-        make_identity(nc, identw[:])
-        b1rows = const.tile([P, 512], BF16, name="b1rows")
-        nc.vector.memset(b1rows[:], 0.0)
         b1cols = const.tile([P, 4, P], BF16, name="b1cols")
         b1T = const.tile([P, 4, 2 * NC], BF16, name="b1T")
         b2b = const.tile([P, NC * D], BF16, name="b2b")
@@ -69,7 +69,12 @@ def tile_patchwork_kernel(tc, tri, W1, b1, W2, b2, gamma, beta, out):
                 return
             if s == 0:
                 t = raw.tile([P, 4, H], BF16, name="raw1", tag="raw1")
-                nc.sync.dma_start(out=t[:], in_=W1[c].rearrange("(p j) h -> p j h", j=4))
+                rows = W1[c].rearrange("(p j) h -> p j h", j=4)
+                if c == 0:
+                    for g in range(2):
+                        nc.sync.dma_start(out=t[:, :, g * 512:(g + 1) * 512], in_=rows[:, :, g * 512:(g + 1) * 512])
+                else:
+                    nc.sync.dma_start(out=t[:], in_=rows)
             else:
                 t = raw.tile([P, 2, 4, D], BF16, name="raw2", tag="raw2")
                 nc.sync.dma_start(out=t[:], in_=W2[c].rearrange("(g p j) d -> p g j d", g=2, j=4))
@@ -103,7 +108,7 @@ def tile_patchwork_kernel(tc, tri, W1, b1, W2, b2, gamma, beta, out):
                 s = w1state["s"]
                 if s < 2 * NC:
                     copy_w1(s // 2, s % 2)
-                if 1 <= s <= 2 * NC:
+                if 2 * (2 + W1_AHEAD) < s <= 2 * NC:
                     quant_w1((s - 1) // 2, (s - 1) % 2)
                 w1state["s"] = s + 1
 
@@ -258,7 +263,12 @@ def tile_patchwork_kernel(tc, tri, W1, b1, W2, b2, gamma, beta, out):
         def round_(i, ln, extra):
             cur = i < NC
             prev = i >= 1
-            if prev:
+            if prev and not cur:
+                quant_h(i - 1, 1)
+                mm2(i - 1)
+                scale_shift_store(ln, i - 2)
+                spread_gb(i - 1)
+            elif prev:
                 spread_gb(i - 1)
                 quant_h(i - 1, 1)
                 mm2(i - 1)
@@ -290,7 +300,8 @@ def tile_patchwork_kernel(tc, tri, W1, b1, W2, b2, gamma, beta, out):
             if prev:
                 quant_w2(i, 2)
                 copy_w2(i + 1, 2)
-                scale_shift_store(ln, i - 1)
+                if i != NC - 1:
+                    scale_shift_store(ln, i - 1)
             if cur:
                 square(i, 1)
             w1_steps(W1Q[i][2])
@@ -309,38 +320,56 @@ def tile_patchwork_kernel(tc, tri, W1, b1, W2, b2, gamma, beta, out):
                     nc.scalar.copy(out=gxs[2 * pair + e][:, bt * 512:(bt + 1) * 512].rearrange("p (b t) -> p b t", t=4),
                                    in_=halves[:, e])
 
-            def quant_x(k):
-                nc.vector.quantize_mx(out=xq[k][:].bitcast(FP8X4), scales=xs[k][:], in_=gxs[k][:])
+            def quant_x(bt, pair):
+                cols = slice(bt * P, (bt + 1) * P)
+                for k in (2 * pair, 2 * pair + 1):
+                    nc.vector.quantize_mx(out=xq[k][:, cols].bitcast(FP8X4), scales=xs[k][:, cols],
+                                          in_=gxs[k][:, bt * 512:(bt + 1) * 512])
 
-            nc.sync.dma_start(out=b1rows[0:2 * NC, :], in_=b1.rearrange("k (g c) -> (k g) c", g=2))
-            for v, vec in enumerate((b2, gamma, beta)):
-                nc.sync.dma_start(out=vrows[v][0:NC, :], in_=vec)
+            make_identity(nc, identw[:])
+            make_identity(nc, ident[:])
             for bt in range(NBT):
                 load_w(bt // 2, bt % 2)
                 nc.sync.dma_start(out=tri_sb[bt][:], in_=tri[bt * P:(bt + 1) * P, :])
+                if bt == 0:
+                    nc.sync.dma_start(out=b1rows[0:2 * NC, :], in_=b1.rearrange("k (g c) -> (k g) c", g=2))
+                    for v, vec in enumerate((b2, gamma, beta)):
+                        nc.sync.dma_start(out=vrows[v][0:NC, :], in_=vec)
             load_w(2, 0)
             load_w(2, 1)
-            nc.vector.tensor_copy(out=b1cols[:], in_=b1rows[:].rearrange("p (m t) -> p t m", t=4))
-            b1p = psum.tile([P, 4, P], BF16, name="b1p", tag="gb", bufs=1)
-            for t in range(4):
-                nc.tensor.transpose(b1p[:, t, :], b1cols[:, t, :], ident[:])
-            nc.scalar.copy(out=b1T[:], in_=b1p[:, :, 0:2 * NC])
-            for kk in range(NC // 2):
-                bb = psum.tile([P, 2, D], BF16, name="bb", tag="acc", bufs=3)
-                spread(bb[:, 0, :], 0, 2 * kk)
-                spread(bb[:, 1, :], 0, 2 * kk + 1)
-                nc.scalar.copy(out=b2b[:, 2 * kk * D:(2 * kk + 2) * D], in_=bb[:].rearrange("p a d -> p (a d)"))
-            for bt in range(NBT):
-                head_v(bt)
-                for pair in range(NC // 2):
-                    xpose(bt, pair)
-            for pair in range(NC // 2):
-                quant_x(2 * pair)
-                quant_x(2 * pair + 1)
-                if pair == 0:
-                    mm1(0, 0)
-                    mm1(0, 1)
-                w1_steps(HEAD_END[pair])
+            todo = []
+            for c in range(2):
+                todo.extend([(copy_w1, c, 0), (copy_w1, c, 1), (quant_w1, c, 0), (quant_w1, c, 1)])
+                if c == 0:
+                    todo.extend([(copy_w2, 0, 0), (copy_w2, 0, 1), (quant_w2, 0, 0), (copy_w2, 0, 2), (quant_w2, 0, 1), (quant_w2, 0, 2)])
+                else:
+                    todo.extend([(copy_w2, 1, 0), (copy_w2, 1, 1), (copy_w2, 1, 2)])
+            for c in range(2, 2 + W1_AHEAD):
+                todo.extend([(copy_w1, c, 0), (copy_w1, c, 1), (quant_w1, c, 0), (quant_w1, c, 1)])
+            tiles = [(bt, pair) for bt in range(NBT) for pair in range(NC // 2)]
+            for n in range(len(tiles) + X_LAG):
+                for fn, c, part in todo[HEAD_RATE * n:HEAD_RATE * (n + 1)]:
+                    fn(c, part)
+                if n < len(tiles):
+                    xpose(tiles[n][0], tiles[n][1])
+                if n == 3:
+                    nc.vector.tensor_copy(out=b1cols[:], in_=b1rows[:].rearrange("p (m t) -> p t m", t=4))
+                    b1p = psum.tile([P, 4, P], BF16, name="b1p", tag="gb", bufs=1)
+                    for t in range(4):
+                        nc.tensor.transpose(b1p[:, t, :], b1cols[:, t, :], ident[:])
+                    nc.scalar.copy(out=b1T[:], in_=b1p[:, :, 0:2 * NC])
+                    for kk in range(NC // 2):
+                        bb = psum.tile([P, 2, D], BF16, name="bb", tag="acc", bufs=3)
+                        spread(bb[:, 0, :], 0, 2 * kk)
+                        spread(bb[:, 1, :], 0, 2 * kk + 1)
+                        nc.scalar.copy(out=b2b[:, 2 * kk * D:(2 * kk + 2) * D], in_=bb[:].rearrange("p a d -> p (a d)"))
+                if n >= X_LAG:
+                    quant_x(tiles[n - X_LAG][0], tiles[n - X_LAG][1])
+            mm1(0, 0)
+            mm1(0, 1)
+            for fn, c, part in todo[HEAD_RATE * (len(tiles) + X_LAG):]:
+                fn(c, part)
+            w1state["s"] = 2 * (2 + W1_AHEAD)
 
         ln = ctx.enter_context(tc.tile_pool(name="ln", bufs=4))
         for i in range(NC + 1):

@@ -22,8 +22,8 @@ G_FROM = 2
 X_HEAD = 2
 XB = False
 RV = ((0, 0), (0, 0), (0, 0), (0, 0), (0, 0), (0, 0), (0, 0), (0, 0))
-W1Q = ((2, 2, 2), (0, 1, 0), (0, 1, 0), (0, 1, 0), (0, 1, 0), (0, 1, 0), (0, 0, 0), (0, 0, 0), (0, 0, 0))
-W1_AHEAD = 1
+W1Q = ((3, 4), (1, 1), (1, 0), (1, 0), (1, 0), (1, 0), (0, 0), (0, 0), (0, 0), (0, 0))
+W1_AHEAD = 0
 HEAD_RATE = 2
 X_LAG = 1
 
@@ -38,7 +38,7 @@ def tile_patchwork_kernel(tc, tri, W1, b1, W2, b2, gamma, beta, out):
         gv = ctx.enter_context(tc.tile_pool(name="gv", bufs=1))
         wq = ctx.enter_context(tc.tile_pool(name="wq", bufs=8))
         hq = ctx.enter_context(tc.tile_pool(name="hq", bufs=4))
-        stats = ctx.enter_context(tc.tile_pool(name="stats", bufs=2))
+        stats = ctx.enter_context(tc.tile_pool(name="stats", bufs=3))
         rp = ctx.enter_context(tc.tile_pool(name="r", bufs=2))
         ghp = ctx.enter_context(tc.tile_pool(name="gh", bufs=2))
         psum = ctx.enter_context(tc.psum_pool(name="psum", bufs=1))
@@ -134,7 +134,7 @@ def tile_patchwork_kernel(tc, tri, W1, b1, W2, b2, gamma, beta, out):
             if c >= NC or c < 0:
                 return
             g, lo, hi = PIECES[piece]
-            if piece != 2:
+            if (c, 1, g) not in wcodes:
                 q = wq.tile([P, 512], U32, name="wcode", tag="w1q", bufs=5, align_bytes=64)
                 sc = wq.tile([P, 512], U8, name="wscale", tag="w1s", bufs=5, align_bytes=64)
                 wcodes[(c, 1, g)] = (q, sc)
@@ -190,11 +190,6 @@ def tile_patchwork_kernel(tc, tri, W1, b1, W2, b2, gamma, beta, out):
         st = {}
         gbs = {}
 
-        def spread_gb(k):
-            gb = psum.tile([P, 2, D], BF16, name="gb", tag="gb", bufs=1)
-            spread(gb[:, 0, :], 1, k)
-            spread(gb[:, 1, :], 2, k)
-            gbs[k] = gb
 
         def mm2(k):
             for bt in range(NBT):
@@ -209,6 +204,7 @@ def tile_patchwork_kernel(tc, tri, W1, b1, W2, b2, gamma, beta, out):
 
         def add_bias(ln, k):
             st[k] = dict((nm, stats.tile([P, NBT], F32, name=nm, tag=nm)) for nm in ("sums", "negmu", "ss", "rstd"))
+            st[k]["unused"] = stats.tile([P, 1], F32, name="unused", tag="unused")
             for bt in range(NBT):
                 y = ln.tile([P, D], F32, name="y", tag="y")
                 nc.vector.scalar_tensor_tensor(out=y[:], in0=accs[(k, bt)][:], scalar=1.0,
@@ -216,7 +212,7 @@ def tile_patchwork_kernel(tc, tri, W1, b1, W2, b2, gamma, beta, out):
                                                accum_out=st[k]["sums"][:, bt:bt + 1])
                 ys[(k, bt)] = y
             nc.vector.tensor_scalar(out=st[k]["negmu"][:], in0=st[k]["sums"][:], scalar1=-1.0 / D, scalar2=0.0,
-                                    op0=ALU.mult, op1=ALU.add)
+                                    op0=ALU.mult, op1=ALU.add, accum_out=st[k]["unused"][:])
 
         def variance(ln, k):
             for bt in range(NBT):
@@ -229,16 +225,16 @@ def tile_patchwork_kernel(tc, tri, W1, b1, W2, b2, gamma, beta, out):
 
         def centre_gain(ln, k):
             for bt in range(NBT):
-                u = ln.tile([P, D], F32, name="u", tag="u")
+                u = ln.tile([P, D], F32, name="u", tag="u", bufs=8)
                 nc.vector.scalar_tensor_tensor(out=u[:], in0=ys[(k, bt)][:], scalar=st[k]["negmu"][:, bt:bt + 1],
-                                               in1=gbs[k][:, 0, :], op0=ALU.add, op1=ALU.mult)
+                                               in1=gbt[:, 0, :], op0=ALU.add, op1=ALU.mult)
                 us[(k, bt)] = u
 
         def scale_shift_store(ln, k):
             for bt in range(NBT):
-                z = ln.tile([P, D], F32, name="z", tag="z")
+                z = ln.tile([P, D], F32, name="z", tag="z", bufs=8)
                 nc.vector.scalar_tensor_tensor(out=z[:], in0=us[(k, bt)][:], scalar=st[k]["rstd"][:, bt:bt + 1],
-                                               in1=gbs[k][:, 1, :], op0=ALU.mult, op1=ALU.add)
+                                               in1=gbt[:, 1, :], op0=ALU.mult, op1=ALU.add)
                 nc.sync.dma_start(out=out[bt * P:(bt + 1) * P, k * D:(k + 1) * D], in_=z[:])
 
         def head_v(bt):
@@ -262,14 +258,10 @@ def tile_patchwork_kernel(tc, tri, W1, b1, W2, b2, gamma, beta, out):
 
         def round_(i, ln, extra):
             cur = i < NC
-            prev = i >= 1
-            if prev and not cur:
-                quant_h(i - 1, 1)
-                mm2(i - 1)
-                scale_shift_store(ln, i - 2)
-                spread_gb(i - 1)
-            elif prev:
-                spread_gb(i - 1)
+            prev = 1 <= i <= NC
+            prev2 = i >= 2
+            if prev:
+                quant_h(i - 1, 0)
                 quant_h(i - 1, 1)
                 mm2(i - 1)
             if cur:
@@ -277,34 +269,31 @@ def tile_patchwork_kernel(tc, tri, W1, b1, W2, b2, gamma, beta, out):
                 mm1(i + 1, 0)
             w1_steps(W1Q[i][0])
             if prev:
-                quant_w2(i, 0)
                 quant_w2(i, 1)
-            relu_v(i, 0)
-            if prev:
+                quant_w2(i, 2)
+                quant_w2(i, 0)
+                copy_w2(i + 1, 0)
+                copy_w2(i + 1, 1)
+                copy_w2(i + 1, 2)
                 add_bias(ln, i - 1)
             if cur:
                 square(i, 0)
             if prev:
-                copy_w2(i + 1, 0)
-                copy_w2(i + 1, 1)
                 centre_gain(ln, i - 1)
+            if prev2:
+                scale_shift_store(ln, i - 2)
+            if i < NC:
+                spread(gbt[:, 0, :], 1, i)
+            if prev:
+                spread(gbt[:, 1, :], 2, i - 1)
             if cur:
                 relu(i, 1)
                 mm1(i + 1, 1)
-            relu_v(i, 1)
             if prev:
                 variance(ln, i - 1)
             if cur:
-                quant_h(i, 0)
-            w1_steps(W1Q[i][1])
-            if prev:
-                quant_w2(i, 2)
-                copy_w2(i + 1, 2)
-                if i != NC - 1:
-                    scale_shift_store(ln, i - 1)
-            if cur:
                 square(i, 1)
-            w1_steps(W1Q[i][2])
+            w1_steps(W1Q[i][1])
 
         with tc.tile_pool(name="tri", bufs=1) as tri_pool:
             tri_sb = [tri_pool.tile([P, NC * APC], BF16, name="tri%d" % bt) for bt in range(NBT)]
@@ -329,8 +318,8 @@ def tile_patchwork_kernel(tc, tri, W1, b1, W2, b2, gamma, beta, out):
             make_identity(nc, identw[:])
             make_identity(nc, ident[:])
             for bt in range(NBT):
-                load_w(bt // 2, bt % 2)
                 nc.sync.dma_start(out=tri_sb[bt][:], in_=tri[bt * P:(bt + 1) * P, :])
+                load_w(bt // 2, bt % 2)
                 if bt == 0:
                     nc.sync.dma_start(out=b1rows[0:2 * NC, :], in_=b1.rearrange("k (g c) -> (k g) c", g=2))
                     for v, vec in enumerate((b2, gamma, beta)):
@@ -372,5 +361,6 @@ def tile_patchwork_kernel(tc, tri, W1, b1, W2, b2, gamma, beta, out):
             w1state["s"] = 2 * (2 + W1_AHEAD)
 
         ln = ctx.enter_context(tc.tile_pool(name="ln", bufs=4))
-        for i in range(NC + 1):
-            round_(i, ln, lambda slot: None)
+        gbt = psum.tile([P, 2, D], BF16, name="gbt", tag="gb", bufs=1)
+        for i in range(NC + 2):
+            round_(i, ln, None)

@@ -188,7 +188,7 @@ def tile_patchwork_kernel(tc, tri, W1, b1, W2, b2, gamma, beta, out):
         ys = {}
         us = {}
         st = {}
-        gbs = {}
+        betas = {}
 
 
         def mm2(k):
@@ -211,8 +211,14 @@ def tile_patchwork_kernel(tc, tri, W1, b1, W2, b2, gamma, beta, out):
                                                in1=b2b[:, k * D:(k + 1) * D], op0=ALU.mult, op1=ALU.add,
                                                accum_out=st[k]["sums"][:, bt:bt + 1])
                 ys[(k, bt)] = y
-            nc.vector.tensor_scalar(out=st[k]["negmu"][:], in0=st[k]["sums"][:], scalar1=-1.0 / D, scalar2=0.0,
-                                    op0=ALU.mult, op1=ALU.add, accum_out=st[k]["unused"][:])
+                if bt == NBT - 1 or (k == NC - 1 and bt == 1):
+                    cols = slice(0, NBT) if k != NC - 1 else slice(bt - 1, bt + 1)
+                    if k + 2 < NC:
+                        nc.vector.tensor_scalar(out=st[k]["negmu"][:, cols], in0=st[k]["sums"][:, cols], scalar1=-1.0 / D,
+                                                scalar2=0.0, op0=ALU.mult, op1=ALU.add, accum_out=st[k]["unused"][:])
+                    else:
+                        nc.vector.tensor_scalar(out=st[k]["negmu"][:, cols], in0=st[k]["sums"][:, cols], scalar1=-1.0 / D,
+                                                scalar2=0.0, op0=ALU.mult, op1=ALU.add)
 
         def variance(ln, k):
             for bt in range(NBT):
@@ -220,8 +226,10 @@ def tile_patchwork_kernel(tc, tri, W1, b1, W2, b2, gamma, beta, out):
                 nc.scalar.activation(out=junk[:], in_=ys[(k, bt)][:], func=ACT.Square,
                                      bias=st[k]["negmu"][:, bt:bt + 1], scale=1.0,
                                      accum_out=st[k]["ss"][:, bt:bt + 1])
-            nc.scalar.activation(out=st[k]["rstd"][:], in_=st[k]["ss"][:], func=ACT.Abs_reciprocal_sqrt,
-                                 bias=eps[:], scale=1.0 / D)
+                if bt == NBT - 1 or (k == NC - 1 and bt == 1):
+                    cols = slice(0, NBT) if k != NC - 1 else slice(bt - 1, bt + 1)
+                    nc.scalar.activation(out=st[k]["rstd"][:, cols], in_=st[k]["ss"][:, cols], func=ACT.Abs_reciprocal_sqrt,
+                                         bias=eps[:], scale=1.0 / D)
 
         def centre_gain(ln, k):
             for bt in range(NBT):
@@ -230,11 +238,11 @@ def tile_patchwork_kernel(tc, tri, W1, b1, W2, b2, gamma, beta, out):
                                                in1=gbt[:, 0, :], op0=ALU.add, op1=ALU.mult)
                 us[(k, bt)] = u
 
-        def scale_shift_store(ln, k):
-            for bt in range(NBT):
+        def scale_shift_store(ln, k, bts=(0, 1, 2, 3)):
+            for bt in bts:
                 z = ln.tile([P, D], F32, name="z", tag="z", bufs=8)
                 nc.vector.scalar_tensor_tensor(out=z[:], in0=us[(k, bt)][:], scalar=st[k]["rstd"][:, bt:bt + 1],
-                                               in1=gbt[:, 1, :], op0=ALU.mult, op1=ALU.add)
+                                               in1=betas.get(k, gbt[:, 1, :]), op0=ALU.mult, op1=ALU.add)
                 nc.sync.dma_start(out=out[bt * P:(bt + 1) * P, k * D:(k + 1) * D], in_=z[:])
 
         def head_v(bt):
@@ -261,12 +269,22 @@ def tile_patchwork_kernel(tc, tri, W1, b1, W2, b2, gamma, beta, out):
             prev = 1 <= i <= NC
             prev2 = i >= 2
             if prev:
-                quant_h(i - 1, 0)
+                if i != NC:
+                    quant_h(i - 1, 0)
                 quant_h(i - 1, 1)
                 mm2(i - 1)
+            if i == NC:
+                last = psum.tile([P, 2, D], BF16, name="lastbeta", tag="h", bufs=4)
+                spread(last[:, 0, :], 2, NC - 1)
+                betas[NC - 1] = last[:, 0, :]
+                scale_shift_store(ln, i - 2, (2, 3))
             if cur:
                 relu(i, 0)
                 mm1(i + 1, 0)
+            if i == NC - 1:
+                last = psum.tile([P, 2, D], BF16, name="lastbeta", tag="h", bufs=4)
+                spread(last[:, 0, :], 2, NC - 2)
+                betas[NC - 2] = last[:, 0, :]
             w1_steps(W1Q[i][0])
             if prev:
                 quant_w2(i, 1)
@@ -280,17 +298,20 @@ def tile_patchwork_kernel(tc, tri, W1, b1, W2, b2, gamma, beta, out):
                 square(i, 0)
             if prev:
                 centre_gain(ln, i - 1)
-            if prev2:
+            if prev2 and i != NC:
                 scale_shift_store(ln, i - 2)
             if i < NC:
                 spread(gbt[:, 0, :], 1, i)
-            if prev:
+            if prev and i < NC - 1:
                 spread(gbt[:, 1, :], 2, i - 1)
             if cur:
                 relu(i, 1)
                 mm1(i + 1, 1)
             if prev:
                 variance(ln, i - 1)
+            if i == NC - 1:
+                quant_h(i, 0)
+                scale_shift_store(ln, i - 1, (0, 1))
             if cur:
                 square(i, 1)
             w1_steps(W1Q[i][1])

@@ -112,7 +112,7 @@ def tile_patchwork_kernel(tc, tri, W1, b1, W2, b2, gamma, beta, out):
                     quant_w1((s - 1) // 2, (s - 1) % 2)
                 w1state["s"] = s + 1
 
-        PIECES = ((0, 0, 512), (1, 0, 256), (1, 256, 512))
+        PIECES = ((0, 0, 512), (1, 0, 512))
 
         def copy_w2(c, piece):
             if c >= NC:
@@ -127,7 +127,7 @@ def tile_patchwork_kernel(tc, tri, W1, b1, W2, b2, gamma, beta, out):
                 nc.vector.tensor_copy(out=t[:].rearrange("p (c i j) -> p c j i", i=4, j=4),
                                       in_=raws[(c, 1)][:, g, :, lo:hi].rearrange("p j (c i) -> p c j i", i=4))
             gws[(c, 1, piece)] = t
-            if piece == 2:
+            if piece == 1:
                 load_w(c + 3, 1)
 
         def quant_w2(c, piece):
@@ -288,11 +288,9 @@ def tile_patchwork_kernel(tc, tri, W1, b1, W2, b2, gamma, beta, out):
             w1_steps(W1Q[i][0])
             if prev:
                 quant_w2(i, 1)
-                quant_w2(i, 2)
                 quant_w2(i, 0)
                 copy_w2(i + 1, 0)
                 copy_w2(i + 1, 1)
-                copy_w2(i + 1, 2)
                 add_bias(ln, i - 1)
             if cur:
                 square(i, 0)
@@ -351,9 +349,9 @@ def tile_patchwork_kernel(tc, tri, W1, b1, W2, b2, gamma, beta, out):
             for c in range(2):
                 todo.extend([(copy_w1, c, 0), (copy_w1, c, 1), (quant_w1, c, 0), (quant_w1, c, 1)])
                 if c == 0:
-                    todo.extend([(copy_w2, 0, 0), (copy_w2, 0, 1), (quant_w2, 0, 0), (copy_w2, 0, 2), (quant_w2, 0, 1), (quant_w2, 0, 2)])
+                    todo.extend([(copy_w2, 0, 0), (copy_w2, 0, 1), (quant_w2, 0, 0), (quant_w2, 0, 1)])
                 else:
-                    todo.extend([(copy_w2, 1, 0), (copy_w2, 1, 1), (copy_w2, 1, 2)])
+                    todo.extend([(copy_w2, 1, 0), (copy_w2, 1, 1)])
             for c in range(2, 2 + W1_AHEAD):
                 todo.extend([(copy_w1, c, 0), (copy_w1, c, 1), (quant_w1, c, 0), (quant_w1, c, 1)])
             tiles = [(bt, pair) for bt in range(NBT) for pair in range(NC // 2)]

@@ -204,7 +204,6 @@ def tile_patchwork_kernel(tc, tri, W1, b1, W2, b2, gamma, beta, out):
 
         def add_bias(ln, k):
             st[k] = dict((nm, stats.tile([P, NBT], F32, name=nm, tag=nm)) for nm in ("sums", "negmu", "ss", "rstd"))
-            st[k]["unused"] = stats.tile([P, 1], F32, name="unused", tag="unused")
             for bt in range(NBT):
                 y = ln.tile([P, D], F32, name="y", tag="y")
                 nc.vector.scalar_tensor_tensor(out=y[:], in0=accs[(k, bt)][:], scalar=1.0,
@@ -213,12 +212,7 @@ def tile_patchwork_kernel(tc, tri, W1, b1, W2, b2, gamma, beta, out):
                 ys[(k, bt)] = y
                 if bt == NBT - 1 or (k == NC - 1 and bt == 1):
                     cols = slice(0, NBT) if k != NC - 1 else slice(bt - 1, bt + 1)
-                    if k + 2 < NC:
-                        nc.vector.tensor_scalar(out=st[k]["negmu"][:, cols], in0=st[k]["sums"][:, cols], scalar1=-1.0 / D,
-                                                scalar2=0.0, op0=ALU.mult, op1=ALU.add, accum_out=st[k]["unused"][:])
-                    else:
-                        nc.vector.tensor_scalar(out=st[k]["negmu"][:, cols], in0=st[k]["sums"][:, cols], scalar1=-1.0 / D,
-                                                scalar2=0.0, op0=ALU.mult, op1=ALU.add)
+                    nc.scalar.activation(out=st[k]["negmu"][:, cols], in_=st[k]["sums"][:, cols], func=ACT.Copy, scale=-1.0 / D)
 
         def variance(ln, k):
             for bt in range(NBT):
@@ -294,10 +288,10 @@ def tile_patchwork_kernel(tc, tri, W1, b1, W2, b2, gamma, beta, out):
                 add_bias(ln, i - 1)
             if cur:
                 square(i, 0)
-            if prev:
-                centre_gain(ln, i - 1)
             if prev2 and i != NC:
                 scale_shift_store(ln, i - 2)
+            if prev:
+                centre_gain(ln, i - 1)
             if i < NC:
                 spread(gbt[:, 0, :], 1, i)
             if prev and i < NC - 1:

@@ -159,9 +159,9 @@ def tile_patchwork_kernel(tc, tri, W1, b1, W2, b2, gamma, beta, out):
                 banks[(k, g, t)] = bank[:, t % 2, :]
 
         def relu(k, g):
-            r = rp.tile([P, 4, B], F32, name="r", tag="r")
+            r = rp.tile([P, B // 4, 4, 4], F32, name="r", tag="r")
             for t in range(4 - RV[k][g]):
-                nc.scalar.activation(out=r[:, t, :], in_=banks[(k, g, t)], func=ACT.Relu,
+                nc.scalar.activation(out=r[:, :, t, :], in_=banks[(k, g, t)].rearrange("p (c i) -> p c i", i=4), func=ACT.Relu,
                                      bias=b1T[:, t, 2 * k + g:2 * k + g + 1], scale=1.0)
             rs[(k, g)] = r
 
@@ -169,13 +169,13 @@ def tile_patchwork_kernel(tc, tri, W1, b1, W2, b2, gamma, beta, out):
             if k >= NC:
                 return
             for t in range(4 - RV[k][g], 4):
-                nc.vector.tensor_scalar(out=rs[(k, g)][:, t, :], in0=banks[(k, g, t)],
+                nc.vector.tensor_scalar(out=rs[(k, g)][:, :, t, :], in0=banks[(k, g, t)].rearrange("p (c i) -> p c i", i=4),
                                         scalar1=b1T[:, t, 2 * k + g:2 * k + g + 1], scalar2=0.0, op0=ALU.add, op1=ALU.max)
 
         def square(k, g):
             t = ghp.tile([P, 4 * B], BF16, name="gh", tag="gh", align_bytes=64)
             nc.scalar.activation(out=t[:].rearrange("p (c i t) -> p c t i", i=4, t=4),
-                                 in_=rs[(k, g)][:].rearrange("p t (c i) -> p c t i", i=4), func=ACT.Square)
+                                 in_=rs[(k, g)][:], func=ACT.Square)
             ghs[(k, g)] = t
 
         def quant_h(k, g):

@@ -22,7 +22,8 @@ G_FROM = 2
 X_HEAD = 2
 XB = False
 RV = ((0, 0), (0, 0), (0, 0), (0, 0), (0, 0), (0, 0), (0, 0), (0, 0))
-W1Q = ((3, 4), (1, 1), (1, 0), (1, 0), (1, 0), (1, 0), (0, 0), (0, 0), (0, 0), (0, 0))
+HEAD_STEPS = 7
+W1Q = ((0, 0), (1, 1), (1, 0), (1, 0), (1, 0), (1, 0), (0, 0), (0, 0), (0, 0), (0, 0))
 W1_AHEAD = 0
 HEAD_RATE = 2
 X_LAG = 1
@@ -31,7 +32,6 @@ X_LAG = 1
 def tile_patchwork_kernel(tc, tri, W1, b1, W2, b2, gamma, beta, out):
     nc = tc.nc
     with ExitStack() as ctx:
-        ctx.enter_context(tc.manual_schedule(engines={mybir.EngineType.DVE, mybir.EngineType.Pool}))
         const = ctx.enter_context(tc.tile_pool(name="const", bufs=1))
         raw = ctx.enter_context(tc.tile_pool(name="raw", bufs=3))
         gw = ctx.enter_context(tc.tile_pool(name="gw", bufs=3))
@@ -273,12 +273,16 @@ def tile_patchwork_kernel(tc, tri, W1, b1, W2, b2, gamma, beta, out):
                 betas[NC - 1] = last[:, 0, :]
                 scale_shift_store(ln, i - 2, (2, 3))
             if cur:
-                relu(i, 0)
                 mm1(i + 1, 0)
+                square(i, 0)
+                relu(i, 1)
+                mm1(i + 1, 1)
             if i == NC - 1:
                 last = psum.tile([P, 2, D], BF16, name="lastbeta", tag="h", bufs=4)
                 spread(last[:, 0, :], 2, NC - 2)
                 betas[NC - 2] = last[:, 0, :]
+            if cur:
+                square(i, 1)
             w1_steps(W1Q[i][0])
             if prev:
                 quant_w2(i, 1)
@@ -286,26 +290,20 @@ def tile_patchwork_kernel(tc, tri, W1, b1, W2, b2, gamma, beta, out):
                 copy_w2(i + 1, 0)
                 copy_w2(i + 1, 1)
                 add_bias(ln, i - 1)
-            if cur:
-                square(i, 0)
             if prev2 and i != NC:
                 scale_shift_store(ln, i - 2)
             if prev:
+                variance(ln, i - 1)
                 centre_gain(ln, i - 1)
             if i < NC:
                 spread(gbt[:, 0, :], 1, i)
             if prev and i < NC - 1:
                 spread(gbt[:, 1, :], 2, i - 1)
-            if cur:
-                relu(i, 1)
-                mm1(i + 1, 1)
-            if prev:
-                variance(ln, i - 1)
+            if i + 1 < NC:
+                relu(i + 1, 0)
             if i == NC - 1:
                 quant_h(i, 0)
                 scale_shift_store(ln, i - 1, (0, 1))
-            if cur:
-                square(i, 1)
             w1_steps(W1Q[i][1])
 
         with tc.tile_pool(name="tri", bufs=1) as tri_pool:
@@ -350,8 +348,6 @@ def tile_patchwork_kernel(tc, tri, W1, b1, W2, b2, gamma, beta, out):
                 todo.extend([(copy_w1, c, 0), (copy_w1, c, 1), (quant_w1, c, 0), (quant_w1, c, 1)])
             tiles = [(bt, pair) for bt in range(NBT) for pair in range(NC // 2)]
             for n in range(len(tiles) + X_LAG):
-                for fn, c, part in todo[HEAD_RATE * n:HEAD_RATE * (n + 1)]:
-                    fn(c, part)
                 if n < len(tiles):
                     xpose(tiles[n][0], tiles[n][1])
                 if n == 3:
@@ -367,12 +363,15 @@ def tile_patchwork_kernel(tc, tri, W1, b1, W2, b2, gamma, beta, out):
                         nc.scalar.copy(out=b2b[:, 2 * kk * D:(2 * kk + 2) * D], in_=bb[:].rearrange("p a d -> p (a d)"))
                 if n >= X_LAG:
                     quant_x(tiles[n - X_LAG][0], tiles[n - X_LAG][1])
+            for fn, c, part in todo:
+                fn(c, part)
             mm1(0, 0)
             mm1(0, 1)
-            for fn, c, part in todo[HEAD_RATE * (len(tiles) + X_LAG):]:
-                fn(c, part)
             w1state["s"] = 2 * (2 + W1_AHEAD)
+            w1_steps(HEAD_STEPS)
 
+        relu(0, 0)
+        ctx.enter_context(tc.manual_schedule(engines={mybir.EngineType.DVE, mybir.EngineType.Pool}))
         ln = ctx.enter_context(tc.tile_pool(name="ln", bufs=4))
         gbt = psum.tile([P, 2, D], BF16, name="gbt", tag="gb", bufs=1)
         for i in range(NC + 2):

@@ -202,9 +202,10 @@ def tile_patchwork_kernel(tc, tri, W1, b1, W2, b2, gamma, beta, out):
                                         rhs=wc[:].bitcast(FP8X4), rhs_scale=ws[:], start=(g == 0), stop=(g == 1))
                 accs[(k, bt)] = acc
 
-        def add_bias(ln, k):
-            st[k] = dict((nm, stats.tile([P, NBT], F32, name=nm, tag=nm)) for nm in ("sums", "negmu", "ss", "rstd"))
-            for bt in range(NBT):
+        def add_bias(ln, k, bts=(0, 1, 2, 3)):
+            if bts[0] == 0:
+                st[k] = dict((nm, stats.tile([P, NBT], F32, name=nm, tag=nm)) for nm in ("sums", "negmu", "ss", "rstd"))
+            for bt in bts:
                 y = ln.tile([P, D], F32, name="y", tag="y")
                 nc.vector.scalar_tensor_tensor(out=y[:], in0=accs[(k, bt)][:], scalar=1.0,
                                                in1=b2b[:, k * D:(k + 1) * D], op0=ALU.mult, op1=ALU.add,
@@ -212,7 +213,11 @@ def tile_patchwork_kernel(tc, tri, W1, b1, W2, b2, gamma, beta, out):
                 ys[(k, bt)] = y
                 if bt == NBT - 1 or (k == NC - 1 and bt == 1):
                     cols = slice(0, NBT) if k != NC - 1 else slice(bt - 1, bt + 1)
-                    nc.scalar.activation(out=st[k]["negmu"][:, cols], in_=st[k]["sums"][:, cols], func=ACT.Copy, scale=-1.0 / D)
+                    if k >= NC - 2:
+                        nc.vector.tensor_scalar(out=st[k]["negmu"][:, cols], in0=st[k]["sums"][:, cols], scalar1=-1.0 / D,
+                                                scalar2=0.0, op0=ALU.mult, op1=ALU.add)
+                    else:
+                        nc.scalar.activation(out=st[k]["negmu"][:, cols], in_=st[k]["sums"][:, cols], func=ACT.Copy, scale=-1.0 / D)
 
         def variance(ln, k):
             for bt in range(NBT):
@@ -271,7 +276,7 @@ def tile_patchwork_kernel(tc, tri, W1, b1, W2, b2, gamma, beta, out):
                 last = psum.tile([P, 2, D], BF16, name="lastbeta", tag="h", bufs=4)
                 spread(last[:, 0, :], 2, NC - 1)
                 betas[NC - 1] = last[:, 0, :]
-                scale_shift_store(ln, i - 2, (2, 3))
+                scale_shift_store(ln, i - 2, (0, 1, 2, 3))
             if cur:
                 mm1(i + 1, 0)
                 square(i, 0)
@@ -289,8 +294,14 @@ def tile_patchwork_kernel(tc, tri, W1, b1, W2, b2, gamma, beta, out):
                 quant_w2(i, 0)
                 copy_w2(i + 1, 0)
                 copy_w2(i + 1, 1)
-                add_bias(ln, i - 1)
-            if prev2 and i != NC:
+                if prev2 and i != NC:
+                    add_bias(ln, i - 1, (0, 1, 2))
+                    scale_shift_store(ln, i - 2, (0, 1))
+                    add_bias(ln, i - 1, (3,))
+                    scale_shift_store(ln, i - 2, (2, 3))
+                else:
+                    add_bias(ln, i - 1)
+            elif prev2 and i != NC:
                 scale_shift_store(ln, i - 2)
             if prev:
                 variance(ln, i - 1)
@@ -303,7 +314,6 @@ def tile_patchwork_kernel(tc, tri, W1, b1, W2, b2, gamma, beta, out):
                 relu(i + 1, 0)
             if i == NC - 1:
                 quant_h(i, 0)
-                scale_shift_store(ln, i - 1, (0, 1))
             w1_steps(W1Q[i][1])
 
         with tc.tile_pool(name="tri", bufs=1) as tri_pool:

@@ -211,7 +211,10 @@ def tile_patchwork_kernel(tc, tri, W1, b1, W2, b2, gamma, beta, out):
                                                in1=b2b[:, k * D:(k + 1) * D], op0=ALU.mult, op1=ALU.add,
                                                accum_out=st[k]["sums"][:, bt:bt + 1])
                 ys[(k, bt)] = y
-                if bt == NBT - 1 or (k == NC - 1 and bt == 1):
+                if k < NC - 2 and bt >= NBT - 2:
+                    cols = slice(0, NBT - 1) if bt == NBT - 2 else slice(NBT - 1, NBT)
+                    nc.scalar.activation(out=st[k]["negmu"][:, cols], in_=st[k]["sums"][:, cols], func=ACT.Copy, scale=-1.0 / D)
+                elif bt == NBT - 1 or (k == NC - 1 and bt == 1):
                     cols = slice(0, NBT) if k != NC - 1 else slice(bt - 1, bt + 1)
                     if k >= NC - 2:
                         nc.vector.tensor_scalar(out=st[k]["negmu"][:, cols], in0=st[k]["sums"][:, cols], scalar1=-1.0 / D,

from contextlib import ExitStack

import concourse.mybir as mybir
from concourse.masks import make_identity

F32 = mybir.dt.float32
BF16 = mybir.dt.bfloat16
U32 = mybir.dt.uint32
U8 = mybir.dt.uint8
FP8X4 = mybir.dt.float8_e4m3fn_x4
ACT = mybir.ActivationFunctionType
ALU = mybir.AluOpType

B, NC, APC, D = 512, 8, 512, 512
H = 2 * D
LN_EPS = 1e-5
P = 128
NBT = B // P
FLOPS = 2 * B * NC * (APC * H + H * D)

G_FROM = 2
X_HEAD = 2
XB = False
RV = ((0, 0), (0, 0), (0, 0), (0, 0), (0, 0), (0, 0), (0, 0), (0, 0))
HEAD_STEPS = 7
W1Q = ((0, 0), (1, 1), (1, 0), (1, 0), (1, 0), (1, 0), (0, 0), (0, 0), (0, 0), (0, 0))
W1_AHEAD = 0
HEAD_RATE = 2
X_LAG = 1


def tile_patchwork_kernel(tc, tri, W1, b1, W2, b2, gamma, beta, out):
    nc = tc.nc
    with ExitStack() as ctx:
        const = ctx.enter_context(tc.tile_pool(name="const", bufs=1))
        raw = ctx.enter_context(tc.tile_pool(name="raw", bufs=3))
        gw = ctx.enter_context(tc.tile_pool(name="gw", bufs=3))
        gv = ctx.enter_context(tc.tile_pool(name="gv", bufs=1))
        wq = ctx.enter_context(tc.tile_pool(name="wq", bufs=8))
        hq = ctx.enter_context(tc.tile_pool(name="hq", bufs=4))
        stats = ctx.enter_context(tc.tile_pool(name="stats", bufs=3))
        rp = ctx.enter_context(tc.tile_pool(name="r", bufs=2))
        ghp = ctx.enter_context(tc.tile_pool(name="gh", bufs=2))
        psum = ctx.enter_context(tc.psum_pool(name="psum", bufs=1))

        b1rows = const.tile([P, 512], BF16, name="b1rows")
        nc.vector.memset(b1rows[:], 0.0)
        vrows = [const.tile([P, D], BF16, name="vrows%d" % v) for v in range(3)]
        for v in range(3):
            nc.vector.memset(vrows[v][:], 0.0)
        eps = const.tile([P, 1], F32, name="eps")
        nc.vector.memset(eps[:], LN_EPS)
        warm = const.tile([P, 1], F32, name="warm")
        nc.scalar.activation(out=warm[:], in_=eps[:], func=ACT.Abs_reciprocal_sqrt)
        ident = const.tile([P, P], BF16, name="ident")
        identw = const.tile([P, P], F32, name="identw")
        b1cols = const.tile([P, 4, P], BF16, name="b1cols")
        b1T = const.tile([P, 4, 2 * NC], BF16, name="b1T")
        b2b = const.tile([P, NC * D], BF16, name="b2b")
        xq = [const.tile([P, B], U32, name="xq%d" % k, align_bytes=64) for k in range(NC)]
        xs = [const.tile([P, B], U8, name="xs%d" % k, align_bytes=64) for k in range(NC)]

        raws = {}
        gws = {}
        wcodes = {}

        def load_w(c, s):
            if c >= NC:
                return
            if s == 0:
                t = raw.tile([P, 4, H], BF16, name="raw1", tag="raw1")
                rows = W1[c].rearrange("(p j) h -> p j h", j=4)
                if c == 0:
                    for g in range(2):
                        nc.sync.dma_start(out=t[:, :, g * 512:(g + 1) * 512], in_=rows[:, :, g * 512:(g + 1) * 512])
                else:
                    nc.sync.dma_start(out=t[:], in_=rows)
            else:
                t = raw.tile([P, 2, 4, D], BF16, name="raw2", tag="raw2")
                nc.sync.dma_start(out=t[:], in_=W2[c].rearrange("(g p j) d -> p g j d", g=2, j=4))
            raws[(c, s)] = t

        def spread(dst, v, row):
            nc.tensor.matmul(out=dst, lhsT=ident[:, row:row + 1].to_broadcast([P, P]), rhs=vrows[v][:], start=True, stop=True)

        def copy_w1(c, g):
            if c >= NC:
                return
            t = gw.tile([P, 2048], BF16, name="gw", tag="gw", align_bytes=64)
            src = raws[(c, 0)][:, :, g * 512:(g + 1) * 512].rearrange("p j (m t) -> p m j t", t=4)
            nc.vector.tensor_copy(out=t[:].rearrange("p (t m j) -> p m j t", t=4, j=4), in_=src)
            gws[(c, 0, g)] = t
            if g == 1:
                load_w(c + 3, 0)

        def quant_w1(c, g):
            if c >= NC:
                return
            q = wq.tile([P, 512], U32, name="wcode", tag="w0q", align_bytes=64)
            sc = wq.tile([P, 512], U8, name="wscale", tag="w0s", align_bytes=64)
            nc.vector.quantize_mx(out=q[:].bitcast(FP8X4), scales=sc[:], in_=gws[(c, 0, g)][:])
            wcodes[(c, 0, g)] = (q, sc)

        w1state = {"s": 0}

        def w1_steps(count):
            for rep_ in range(count):
                s = w1state["s"]
                if s < 2 * NC:
                    copy_w1(s // 2, s % 2)
                if 2 * (2 + W1_AHEAD) < s <= 2 * NC:
                    quant_w1((s - 1) // 2, (s - 1) % 2)
                w1state["s"] = s + 1

        PIECES = ((0, 0, 512), (1, 0, 512))

        def copy_w2(c, piece):
            if c >= NC:
                return
            g, lo, hi = PIECES[piece]
            t = gv.tile([P, 4 * (hi - lo)], BF16, name="gv%d" % piece, tag="gv%d" % piece, align_bytes=64)
            if c >= G_FROM:
                nc.gpsimd.tensor_scalar(out=t[:].rearrange("p (d j) -> p d j", j=4),
                                        in0=raws[(c, 1)][:, g, :, lo:hi].rearrange("p j d -> p d j"),
                                        scalar1=1.0, scalar2=0.0, op0=ALU.mult, op1=ALU.add)
            else:
                nc.vector.tensor_copy(out=t[:].rearrange("p (c i j) -> p c j i", i=4, j=4),
                                      in_=raws[(c, 1)][:, g, :, lo:hi].rearrange("p j (c i) -> p c j i", i=4))
            gws[(c, 1, piece)] = t
            if piece == 1:
                load_w(c + 3, 1)

        def quant_w2(c, piece):
            if c >= NC or c < 0:
                return
            g, lo, hi = PIECES[piece]
            if (c, 1, g) not in wcodes:
                q = wq.tile([P, 512], U32, name="wcode", tag="w1q", bufs=5, align_bytes=64)
                sc = wq.tile([P, 512], U8, name="wscale", tag="w1s", bufs=5, align_bytes=64)
                wcodes[(c, 1, g)] = (q, sc)
            q, sc = wcodes[(c, 1, g)]
            nc.vector.quantize_mx(out=q[:, lo:hi].bitcast(FP8X4), scales=sc[:, lo:hi], in_=gws[(c, 1, piece)][:])

        banks = {}
        rs = {}
        ghs = {}
        hcodes = {}

        def mm1(k, g):
            if k >= NC:
                return
            q, sc = wcodes[(k, 0, g)]
            for t in range(4):
                if t % 2 == 0:
                    bank = psum.tile([P, 2, B], BF16, name="hbank", tag="h", bufs=4)
                cols = slice(t * P, (t + 1) * P)
                nc.tensor.matmul_mx(out=bank[:, t % 2, :], lhsT=q[:, cols].bitcast(FP8X4), lhsT_scale=sc[:, cols],
                                    rhs=xq[k][:].bitcast(FP8X4), rhs_scale=xs[k][:], start=True, stop=True)
                banks[(k, g, t)] = bank[:, t % 2, :]

        def relu(k, g):
            r = rp.tile([P, B // 4, 4, 4], F32, name="r", tag="r")
            for t in range(4 - RV[k][g]):
                nc.scalar.activation(out=r[:, :, t, :], in_=banks[(k, g, t)].rearrange("p (c i) -> p c i", i=4), func=ACT.Relu,
                                     bias=b1T[:, t, 2 * k + g:2 * k + g + 1], scale=1.0)
            rs[(k, g)] = r

        def relu_v(k, g):
            if k >= NC:
                return
            for t in range(4 - RV[k][g], 4):
                nc.vector.tensor_scalar(out=rs[(k, g)][:, :, t, :], in0=banks[(k, g, t)].rearrange("p (c i) -> p c i", i=4),
                                        scalar1=b1T[:, t, 2 * k + g:2 * k + g + 1], scalar2=0.0, op0=ALU.add, op1=ALU.max)

        def square(k, g):
            t = ghp.tile([P, 4 * B], BF16, name="gh", tag="gh", align_bytes=64)
            nc.scalar.activation(out=t[:].rearrange("p (c i t) -> p c t i", i=4, t=4),
                                 in_=rs[(k, g)][:], func=ACT.Square)
            ghs[(k, g)] = t

        def quant_h(k, g):
            q = hq.tile([P, B], U32, name="hcode", tag="hq", align_bytes=64)
            sc = hq.tile([P, B], U8, name="hscale", tag="hs", align_bytes=64)
            nc.vector.quantize_mx(out=q[:].bitcast(FP8X4), scales=sc[:], in_=ghs[(k, g)][:])
            hcodes[(k, g)] = (q, sc)

        accs = {}
        ys = {}
        us = {}
        st = {}
        betas = {}


        def mm2(k):
            for bt in range(NBT):
                acc = psum.tile([P, D], F32, name="acc", tag="acc", bufs=3)
                cols = slice(bt * P, (bt + 1) * P)
                for g in range(2):
                    q, sc = hcodes[(k, g)]
                    wc, ws = wcodes[(k, 1, g)]
                    nc.tensor.matmul_mx(out=acc[:], lhsT=q[:, cols].bitcast(FP8X4), lhsT_scale=sc[:, cols],
                                        rhs=wc[:].bitcast(FP8X4), rhs_scale=ws[:], start=(g == 0), stop=(g == 1))
                accs[(k, bt)] = acc

        def add_bias(ln, k, bts=(0, 1, 2, 3)):
            if bts[0] == 0:
                st[k] = dict((nm, stats.tile([P, NBT], F32, name=nm, tag=nm)) for nm in ("sums", "negmu", "ss", "rstd"))
            for bt in bts:
                y = ln.tile([P, D], F32, name="y", tag="y")
                nc.vector.scalar_tensor_tensor(out=y[:], in0=accs[(k, bt)][:], scalar=1.0,
                                               in1=b2b[:, k * D:(k + 1) * D], op0=ALU.mult, op1=ALU.add,
                                               accum_out=st[k]["sums"][:, bt:bt + 1])
                ys[(k, bt)] = y
                if k < NC - 2 and bt >= NBT - 2:
                    cols = slice(0, NBT - 1) if bt == NBT - 2 else slice(NBT - 1, NBT)
                    nc.scalar.activation(out=st[k]["negmu"][:, cols], in_=st[k]["sums"][:, cols], func=ACT.Copy, scale=-1.0 / D)
                elif bt == NBT - 1 or (k == NC - 1 and bt == 1):
                    cols = slice(0, NBT) if k != NC - 1 else slice(bt - 1, bt + 1)
                    if k >= NC - 2:
                        nc.vector.tensor_scalar(out=st[k]["negmu"][:, cols], in0=st[k]["sums"][:, cols], scalar1=-1.0 / D,
                                                scalar2=0.0, op0=ALU.mult, op1=ALU.add)
                    else:
                        nc.scalar.activation(out=st[k]["negmu"][:, cols], in_=st[k]["sums"][:, cols], func=ACT.Copy, scale=-1.0 / D)

        def variance(ln, k):
            for bt in range(NBT):
                junk = ln.tile([P, D], BF16, name="junk", tag="junk", bufs=2)
                nc.scalar.activation(out=junk[:], in_=ys[(k, bt)][:], func=ACT.Square,
                                     bias=st[k]["negmu"][:, bt:bt + 1], scale=1.0,
                                     accum_out=st[k]["ss"][:, bt:bt + 1])
                if bt == NBT - 1 or (k == NC - 1 and bt == 1):
                    cols = slice(0, NBT) if k != NC - 1 else slice(bt - 1, bt + 1)
                    nc.scalar.activation(out=st[k]["rstd"][:, cols], in_=st[k]["ss"][:, cols], func=ACT.Abs_reciprocal_sqrt,
                                         bias=eps[:], scale=1.0 / D)

        def centre_gain(ln, k):
            for bt in range(NBT):
                u = ln.tile([P, D], F32, name="u", tag="u", bufs=8)
                nc.vector.scalar_tensor_tensor(out=u[:], in0=ys[(k, bt)][:], scalar=st[k]["negmu"][:, bt:bt + 1],
                                               in1=gbt[:, 0, :], op0=ALU.add, op1=ALU.mult)
                us[(k, bt)] = u

        def scale_shift_store(ln, k, bts=(0, 1, 2, 3)):
            for bt in bts:
                z = ln.tile([P, D], F32, name="z", tag="z", bufs=8)
                nc.vector.scalar_tensor_tensor(out=z[:], in0=us[(k, bt)][:], scalar=st[k]["rstd"][:, bt:bt + 1],
                                               in1=betas.get(k, gbt[:, 1, :]), op0=ALU.mult, op1=ALU.add)
                nc.sync.dma_start(out=out[bt * P:(bt + 1) * P, k * D:(k + 1) * D], in_=z[:])

        def head_v(bt):
            if bt == 0:
                w1_steps(2)
            elif bt == 1:
                copy_w2(0, 0)
                copy_w2(0, 1)
                quant_w2(0, 0)
                copy_w2(0, 2)
                quant_w2(0, 1)
            elif bt == 2:
                w1_steps(1)
                quant_w2(0, 2)
                w1_steps(1)
            else:
                copy_w2(1, 0)
                w1_steps(1)
                copy_w2(1, 1)
                copy_w2(1, 2)

        def round_(i, ln, extra):
            cur = i < NC
            prev = 1 <= i <= NC
            prev2 = i >= 2
            if prev:
                if i != NC:
                    quant_h(i - 1, 0)
                quant_h(i - 1, 1)
                mm2(i - 1)
            if i == NC:
                last = psum.tile([P, 2, D], BF16, name="lastbeta", tag="h", bufs=4)
                spread(last[:, 0, :], 2, NC - 1)
                betas[NC - 1] = last[:, 0, :]
                scale_shift_store(ln, i - 2, (0, 1, 2, 3))
            if cur:
                mm1(i + 1, 0)
                square(i, 0)
                relu(i, 1)
                mm1(i + 1, 1)
            if i == NC - 1:
                last = psum.tile([P, 2, D], BF16, name="lastbeta", tag="h", bufs=4)
                spread(last[:, 0, :], 2, NC - 2)
                betas[NC - 2] = last[:, 0, :]
            if cur:
                square(i, 1)
            w1_steps(W1Q[i][0])
            if prev:
                quant_w2(i, 1)
                quant_w2(i, 0)
                copy_w2(i + 1, 0)
                copy_w2(i + 1, 1)
                if prev2 and i != NC:
                    add_bias(ln, i - 1, (0, 1, 2))
                    scale_shift_store(ln, i - 2, (0, 1))
                    add_bias(ln, i - 1, (3,))
                    scale_shift_store(ln, i - 2, (2, 3))
                else:
                    add_bias(ln, i - 1)
            elif prev2 and i != NC:
                scale_shift_store(ln, i - 2)
            if prev:
                variance(ln, i - 1)
                centre_gain(ln, i - 1)
            if i < NC:
                spread(gbt[:, 0, :], 1, i)
            if prev and i < NC - 1:
                spread(gbt[:, 1, :], 2, i - 1)
            if i + 1 < NC:
                relu(i + 1, 0)
            if i == NC - 1:
                quant_h(i, 0)
            w1_steps(W1Q[i][1])

        with tc.tile_pool(name="tri", bufs=1) as tri_pool:
            tri_sb = [tri_pool.tile([P, NC * APC], BF16, name="tri%d" % bt) for bt in range(NBT)]
            gxs = [tri_pool.tile([P, 4 * B], BF16, name="gx%d" % k, align_bytes=64) for k in range(NC)]

            def xpose(bt, pair):
                words = tri_sb[bt][:].bitcast(F32)
                xt = psum.tile([P, 4, P], F32, name="xt", tag="h", bufs=4)
                for t in range(4):
                    nc.tensor.transpose(xt[:, t, :], words[:, 4 * t + pair::16], identw[:])
                halves = xt[:].rearrange("p t b -> p (t b)").bitcast(BF16).rearrange("p (t b e) -> p e b t", t=4, e=2)
                for e in range(2):
                    nc.scalar.copy(out=gxs[2 * pair + e][:, bt * 512:(bt + 1) * 512].rearrange("p (b t) -> p b t", t=4),
                                   in_=halves[:, e])

            def quant_x(bt, pair):
                cols = slice(bt * P, (bt + 1) * P)
                for k in (2 * pair, 2 * pair + 1):
                    nc.vector.quantize_mx(out=xq[k][:, cols].bitcast(FP8X4), scales=xs[k][:, cols],
                                          in_=gxs[k][:, bt * 512:(bt + 1) * 512])

            make_identity(nc, identw[:])
            make_identity(nc, ident[:])
            for bt in range(NBT):
                nc.sync.dma_start(out=tri_sb[bt][:], in_=tri[bt * P:(bt + 1) * P, :])
                load_w(bt // 2, bt % 2)
                if bt == 0:
                    nc.sync.dma_start(out=b1rows[0:2 * NC, :], in_=b1.rearrange("k (g c) -> (k g) c", g=2))
                    for v, vec in enumerate((b2, gamma, beta)):
                        nc.sync.dma_start(out=vrows[v][0:NC, :], in_=vec)
            load_w(2, 0)
            load_w(2, 1)
            todo = []
            for c in range(2):
                todo.extend([(copy_w1, c, 0), (copy_w1, c, 1), (quant_w1, c, 0), (quant_w1, c, 1)])
                if c == 0:
                    todo.extend([(copy_w2, 0, 0), (copy_w2, 0, 1), (quant_w2, 0, 0), (quant_w2, 0, 1)])
                else:
                    todo.extend([(copy_w2, 1, 0), (copy_w2, 1, 1)])
            for c in range(2, 2 + W1_AHEAD):
                todo.extend([(copy_w1, c, 0), (copy_w1, c, 1), (quant_w1, c, 0), (quant_w1, c, 1)])
            tiles = [(bt, pair) for bt in range(NBT) for pair in range(NC // 2)]
            for n in range(len(tiles) + X_LAG):
                if n < len(tiles):
                    xpose(tiles[n][0], tiles[n][1])
                if n == 3:
                    nc.vector.tensor_copy(out=b1cols[:], in_=b1rows[:].rearrange("p (m t) -> p t m", t=4))
                    b1p = psum.tile([P, 4, P], BF16, name="b1p", tag="gb", bufs=1)
                    for t in range(4):
                        nc.tensor.transpose(b1p[:, t, :], b1cols[:, t, :], ident[:])
                    nc.scalar.copy(out=b1T[:], in_=b1p[:, :, 0:2 * NC])
                    for kk in range(NC // 2):
                        bb = psum.tile([P, 2, D], BF16, name="bb", tag="acc", bufs=3)
                        spread(bb[:, 0, :], 0, 2 * kk)
                        spread(bb[:, 1, :], 0, 2 * kk + 1)
                        nc.scalar.copy(out=b2b[:, 2 * kk * D:(2 * kk + 2) * D], in_=bb[:].rearrange("p a d -> p (a d)"))
                if n >= X_LAG:
                    quant_x(tiles[n - X_LAG][0], tiles[n - X_LAG][1])
            for fn, c, part in todo:
                fn(c, part)
            mm1(0, 0)
            mm1(0, 1)
            w1state["s"] = 2 * (2 + W1_AHEAD)
            w1_steps(HEAD_STEPS)

        relu(0, 0)
        ctx.enter_context(tc.manual_schedule(engines={mybir.EngineType.DVE, mybir.EngineType.Pool}))
        ln = ctx.enter_context(tc.tile_pool(name="ln", bufs=4))
        gbt = psum.tile([P, 2, D], BF16, name="gbt", tag="gb", bufs=1)
        for i in range(NC + 2):
            round_(i, ln, None)
